import numpy as np
import ml_dtypes


def mxq(x, axis, fmt="e4m3"):
    dtype, down = {"e4m3": (ml_dtypes.float8_e4m3fn, 7), "e5m2": (ml_dtypes.float8_e5m2, 14)}[fmt]
    v = np.moveaxis(np.asarray(x, np.float32).astype(ml_dtypes.bfloat16).astype(np.float64), axis, -1)
    blocks = v.reshape(v.shape[:-1] + (-1, 32))
    amax = np.abs(blocks).max(-1, keepdims=True)
    byte = np.maximum(np.where(amax > 0, np.frexp(amax)[1] - 1 + 127, 0) - down, 1)
    scale = np.exp2(byte - 127.0)
    codes = (blocks / scale).astype(np.float32).astype(dtype).astype(np.float64)
    return np.moveaxis((codes * scale).reshape(v.shape), -1, axis)


WIDE = False


def mx_kscale(k):
    if not WIDE:
        return np.ones(k)
    levels = np.array([10, -10, 5, -5, 0])
    if k % 512:
        return np.exp2(np.random.permutation(np.resize(levels, k // 32))).repeat(32)
    a = np.empty((k // 512, 16))
    for p in range(k // 512):
        a[p, :8] = np.random.permutation(np.resize(levels, 8))
        for g in range(8):
            far = levels[np.abs(levels - a[p, g]) >= 10]
            a[p, g + 8] = far[np.random.randint(len(far))]
    return np.exp2(a.ravel()).repeat(32)


BF16 = ml_dtypes.bfloat16


def bf(x):
    return np.asarray(x, np.float32).astype(BF16)


def f64(x):
    return np.asarray(x).astype(np.float64)


E2M1 = np.array([0.0, 0.5, 1.0, 1.5, 2.0, 3.0, 4.0, 6.0, -0.0, -0.5, -1.0, -1.5, -2.0, -3.0, -4.0, -6.0])


def pack_weight(w, fmt):
    k, n = w.shape
    w = f64(bf(w)).reshape(k // 32, 32, n)
    amax = np.abs(w).max(1)
    if fmt == "e4m3":
        byte = np.frexp(amax)[1] - 1 + 127 - 7
    else:
        mant, ex = np.frexp(amax / 6.0)
        byte = np.where(mant > 0.5, ex, ex - 1) + 127
    byte = np.clip(np.where(amax > 0, byte, 1), 1, 254)
    scaled = (w * np.exp2(127.0 - byte)[:, None, :]).reshape(k, n).astype(np.float32)
    by_word = np.ascontiguousarray(scaled.reshape(k // 512, 128, 4, n).transpose(0, 1, 3, 2))
    if fmt == "e4m3":
        words = by_word.astype(ml_dtypes.float8_e4m3fn).view(np.uint8)
    else:
        c = by_word.astype(ml_dtypes.float4_e2m1fn).view(np.uint8) & 0xF
        words = c[..., 0::2] | (c[..., 1::2] << 4)
    return np.ascontiguousarray(words), np.ascontiguousarray(byte.astype(np.uint8).reshape(k // 512, 16, n))


def unpack_weight(words, scales, fmt):
    g, p, n, _ = words.shape
    if fmt == "e4m3":
        vals = np.ascontiguousarray(words).view(ml_dtypes.float8_e4m3fn).astype(np.float64)
    else:
        nib = np.empty((g, p, n, 4), np.uint8)
        nib[..., 0::2] = words & 0xF
        nib[..., 1::2] = words >> 4
        vals = E2M1[nib]
    vals = vals * np.repeat(np.exp2(scales.astype(np.float64) - 127.0), 8, axis=1)[..., None]
    return vals.transpose(0, 1, 3, 2).reshape(g * 512, n)

def pack4(w):
    words, scales = pack_weight(w, "e2m1")
    return words.reshape(words.shape[0], 128, -1), scales


def unpack4(words, scales):
    return unpack_weight(words.reshape(words.shape[0], 128, -1, 2), scales, "e2m1")


B, D, H = 128, 1024, 2048
G = 4
QH = H % 512 == 0


def sigmoid(v):
    return 1.0 / (1.0 + np.exp(-v))


def setup_inputs():
    s = mx_kscale(D)
    t = mx_kscale(H) if QH else np.ones(H)
    x_t = bf(np.random.standard_normal((B, D)) * s)
    h_pre = bf(np.random.standard_normal((B, H)) * t)
    c_pre = bf(np.random.standard_normal((B, H)))
    Wx = np.random.standard_normal((G, H, D)) * 0.64 / np.sqrt(D) / s
    Wx_cat = np.ascontiguousarray(Wx.swapaxes(1, 2)).reshape(-1, H)
    Wx_words, Wx_scales = pack4(Wx_cat)
    bW = bf(np.random.standard_normal((4, H)) * 0.3)
    Uh = bf(np.random.standard_normal((4, H, H)) * 0.64 / np.sqrt(H) / t)
    bU = bf(np.random.standard_normal((4, H)) * 0.3)
    return {
        "x_t": x_t,
        "h_pre": h_pre,
        "c_pre": c_pre,
        "Wx_words": Wx_words,
        "Wx_scales": Wx_scales,
        "bW": bW,
        "Uh": Uh,
        "bU": bU,
    }


def reference(x_t, h_pre, c_pre, Wx_words, Wx_scales, bW, Uh, bU):
    zx = mxq(f64(x_t), 1, "e4m3") @ unpack4(Wx_words, Wx_scales).reshape(G, D, H)
    if QH:
        zh = mxq(f64(h_pre), 1, "e4m3") @ mxq(f64(Uh), 2, "e4m3").transpose(0, 2, 1)
    else:
        zh = f64(h_pre) @ f64(Uh).transpose(0, 2, 1)
    z = zx + zh + (f64(bW) + f64(bU))[:, None, :]
    f_t = sigmoid(z[0])
    i_t = sigmoid(z[1])
    o_t = sigmoid(z[2])
    g_t = np.tanh(z[3])
    c_t = f_t * f64(c_pre) + i_t * g_t
    h_t = o_t * np.tanh(c_t)
    return (h_t, c_t)

@@ -1,0 +1,337 @@
+from contextlib import ExitStack
+
+import concourse.mybir as mybir
+from concourse.masks import make_identity
+
+F32 = mybir.dt.float32
+BF16 = mybir.dt.bfloat16
+I32 = mybir.dt.int32
+U32 = mybir.dt.uint32
+U8 = mybir.dt.uint8
+FP8X4 = mybir.dt.float8_e4m3fn_x4
+FP4X4 = mybir.dt.float4_e2m1fn_x4
+ACT = mybir.ActivationFunctionType
+ALU = mybir.AluOpType
+
+P = 128
+D = 1024
+H = 2048
+GATES = 4
+K_PASS = 512
+X_PASSES = D // K_PASS
+H_PASSES = H // K_PASS
+WORDS_PER_PASS = K_PASS // 2
+
+N_TILE = 512
+CHUNKS = H // N_TILE
+UNITS = GATES * CHUNKS
+ROWS_PER_PARTITION = 2
+PIECE_ROWS = P * ROWS_PER_PARTITION
+PIECES_PER_UNIT = N_TILE // PIECE_ROWS
+PIECES = UNITS * PIECES_PER_UNIT
+PIECES_PER_GATE = PIECES // GATES
+
+GATE_ORDER = (3, 1, 0, 2)
+STEP_G, STEP_I, STEP_F, STEP_O = 0, 1, 2, 3
+
+RAW_BUFS = 8
+TRANSPOSE_BANKS = 7
+SCALAR_BANKS = 3
+
+FLOPS = 2 * P * (D + H) * GATES * H
+
+
+def tile_lstmcell_w_e_kernel(
+    tc, x_t, h_pre, c_pre, Wx_words, Wx_scales, bW, Uh, bU, out_0, out_1
+):
+    nc = tc.nc
+    with ExitStack() as ctx:
+        ctx.enter_context(tc.manual_schedule())
+        const = ctx.enter_context(tc.tile_pool(name="const", bufs=1))
+        raw_pool = ctx.enter_context(tc.tile_pool(name="raw", bufs=RAW_BUFS))
+        grouped_pool = ctx.enter_context(tc.tile_pool(name="grouped", bufs=2 * H_PASSES))
+        codes_pool = ctx.enter_context(tc.tile_pool(name="codes", bufs=2))
+        wx_pool = ctx.enter_context(tc.tile_pool(name="wx", bufs=2))
+        work = ctx.enter_context(tc.tile_pool(name="work", bufs=2))
+        bias_pool = ctx.enter_context(tc.tile_pool(name="bias", bufs=2 * CHUNKS))
+        banks = ctx.enter_context(tc.psum_pool(name="banks", bufs=TRANSPOSE_BANKS))
+        z_pool = ctx.enter_context(tc.psum_pool(name="z", bufs=1))
+
+        ident = const.tile([P, P], F32)
+        make_identity(nc, ident[:])
+
+        bias_rows = const.tile([P, N_TILE], BF16)
+        nc.vector.memset(bias_rows[:], 0.0)
+        wx_planes = const.tile([P, GATES * X_PASSES, H], U8, align_bytes=64)
+        nc.vector.memset(wx_planes[:].bitcast(I32), 0)
+        pick = const.tile([P, UNITS], BF16)
+        nc.vector.tensor_tensor(
+            out=pick[:], in0=ident[:, 0:UNITS], in1=ident[:, UNITS : 2 * UNITS], op=ALU.add
+        )
+
+        h_raw = const.tile([P, H], BF16)
+        nc.sync.dma_start(out=h_raw[:], in_=h_pre[:, :])
+        x_raw = const.tile([P, D], BF16)
+        nc.sync.dma_start(out=x_raw[:], in_=x_t[:, :])
+        nc.sync.dma_start(
+            out=bias_rows[0:UNITS, :], in_=bW.rearrange("e (c n) -> (e c) n", n=N_TILE)
+        )
+        nc.sync.dma_start(
+            out=bias_rows[UNITS : 2 * UNITS, :], in_=bU.rearrange("e (c n) -> (e c) n", n=N_TILE)
+        )
+        c_old = const.tile([P, H], BF16)
+
+        warm = const.tile([P, 1], F32)
+        nc.scalar.activation(out=warm[:], in_=ident[:, 0:1], func=ACT.Sigmoid)
+
+        cell = const.tile([P, H], F32)
+        tanh_cell = const.tile([P, H], F32)
+
+        raw_of = {}
+        grouped_of = {}
+        codes_of = {}
+        scales_of = {}
+        wx_words_of = {}
+        bias_bank_of = {}
+        bias_of = {}
+        z_of = {}
+        z_biased_of = {}
+        gate_of = {}
+
+        def unit_place(unit):
+            step, chunk = divmod(unit, CHUNKS)
+            return step, GATE_ORDER[step], chunk * N_TILE
+
+        def load_piece(piece):
+            step, rest = divmod(piece, PIECES_PER_GATE)
+            rows = slice(rest * PIECE_ROWS, (rest + 1) * PIECE_ROWS)
+            raw = raw_pool.tile([P, ROWS_PER_PARTITION, H], BF16)
+            nc.sync.dma_start(
+                out=raw[:],
+                in_=Uh[GATE_ORDER[step], rows, :].rearrange(
+                    "(p t) k -> p t k", t=ROWS_PER_PARTITION
+                ),
+            )
+            raw_of[piece] = raw
+
+        def load_gate_weights(step):
+            first = GATE_ORDER[step] * X_PASSES
+            groups = slice(first, first + X_PASSES)
+            for quadrant in range(4):
+                nc.sync.dma_start(
+                    out=wx_planes[32 * quadrant : 32 * quadrant + 4, groups, :].bitcast(I32),
+                    in_=Wx_scales[groups, 4 * quadrant : 4 * quadrant + 4, :]
+                    .bitcast(I32)
+                    .rearrange("g r w -> r g w"),
+                )
+            wx_words = wx_pool.tile([P, X_PASSES, 2 * H], U8, align_bytes=64)
+            nc.sync.dma_start(
+                out=wx_words[:].bitcast(I32),
+                in_=Wx_words[groups, :, :].bitcast(I32).rearrange("g p w -> p g w"),
+            )
+            wx_words_of[step] = wx_words
+
+        def quantise_activations(raw, passes, codes, scales, grouped):
+            raw_words = raw[:].bitcast(F32)
+            grouped_words = grouped[:].bitcast(F32).rearrange(
+                "q (g b u) -> q g b u", g=passes, u=2
+            )
+            for pair in range(passes // 2):
+                bank = banks.tile([P, 4, P], F32)
+                for g in range(2):
+                    for u in range(2):
+                        nc.tensor.transpose(
+                            out=bank[:, 2 * g + u, :],
+                            in_=raw_words[:, word_columns(2 * pair + g, u)],
+                            identity=ident[:],
+                        )
+                nc.scalar.copy(
+                    out=grouped_words[:, 2 * pair : 2 * pair + 2, :, :],
+                    in_=bank[:].rearrange("q (g u) b -> q g b u", u=2),
+                )
+            nc.vector.quantize_mx(
+                out=codes[:].rearrange("q g b -> q (g b)").bitcast(FP8X4),
+                scales=scales[:].rearrange("q g b -> q (g b)"),
+                in_=grouped[:],
+            )
+
+        h_codes = const.tile([P, H_PASSES, P], U32, align_bytes=64)
+        h_scales = const.tile([P, H_PASSES, P], U8, align_bytes=64)
+        h_grouped = const.tile([P, H_PASSES * P * 4], BF16, align_bytes=64)
+        x_codes = const.tile([P, X_PASSES, P], U32, align_bytes=64)
+        x_scales = const.tile([P, X_PASSES, P], U8, align_bytes=64)
+        x_grouped = const.tile([P, X_PASSES * P * 4], BF16, align_bytes=64)
+
+        def word_columns(g, u):
+            return slice(WORDS_PER_PASS * g + u, WORDS_PER_PASS * (g + 1), 2)
+
+        def transpose_piece(piece):
+            raw_words = raw_of[piece][:].bitcast(F32)
+            for g in range(H_PASSES):
+                bank = banks.tile([P, 4, P], F32)
+                for t in range(ROWS_PER_PARTITION):
+                    for u in range(2):
+                        nc.tensor.transpose(
+                            out=bank[:, 2 * t + u, :],
+                            in_=raw_words[:, t, word_columns(g, u)],
+                            identity=ident[:],
+                        )
+                grouped = grouped_pool.tile([P, PIECE_ROWS * 4], BF16, align_bytes=64)
+                copy = nc.scalar.copy if g < SCALAR_BANKS else nc.vector.tensor_copy
+                copy(
+                    out=grouped[:].bitcast(F32).rearrange("q (p c) -> q p c", c=4),
+                    in_=bank[:].rearrange("q c p -> q p c"),
+                )
+                grouped_of[(piece, g)] = grouped
+
+        def quantise_piece(piece):
+            unit, half = divmod(piece, PIECES_PER_UNIT)
+            if half == 0:
+                codes = codes_pool.tile([P, H_PASSES, N_TILE], U32, align_bytes=64)
+                scales = codes_pool.tile([P, H_PASSES, N_TILE], U8, align_bytes=64)
+                codes_of[unit] = codes
+                scales_of[unit] = scales
+            columns = slice(half * PIECE_ROWS, (half + 1) * PIECE_ROWS)
+            for g in range(H_PASSES):
+                nc.vector.quantize_mx(
+                    out=codes_of[unit][:, g, columns].bitcast(FP8X4),
+                    scales=scales_of[unit][:, g, columns],
+                    in_=grouped_of[(piece, g)][:],
+                )
+
+        def spread_bias(unit):
+            step, gate, first = unit_place(unit)
+            row = gate * CHUNKS + first // N_TILE
+            bank = banks.tile([P, 4, P], F32)
+            nc.tensor.matmul(
+                out=bank[:].rearrange("q c p -> q (c p)"),
+                lhsT=pick[:, row : row + 1].to_broadcast([P, P]),
+                rhs=bias_rows[:],
+                start=True,
+                stop=True,
+            )
+            bias_bank_of[unit] = bank
+
+        def fetch_bias(unit):
+            bias = bias_pool.tile([P, N_TILE], F32)
+            nc.scalar.copy(out=bias[:], in_=bias_bank_of[unit][:].rearrange("q c p -> q (c p)"))
+            bias_of[unit] = bias
+
+        def multiply(unit):
+            step, gate, first = unit_place(unit)
+            z = z_pool.tile([P, N_TILE], F32)
+            for g in range(X_PASSES):
+                nc.tensor.matmul_mx(
+                    out=z[:],
+                    lhsT=x_codes[:, g, :].bitcast(FP8X4),
+                    lhsT_scale=x_scales[:, g, :],
+                    rhs=wx_words_of[step][:, g, 2 * first : 2 * (first + N_TILE)].bitcast(FP4X4),
+                    rhs_scale=wx_planes[:, gate * X_PASSES + g, first : first + N_TILE],
+                    start=(g == 0),
+                    stop=False,
+                )
+            for g in range(H_PASSES):
+                nc.tensor.matmul_mx(
+                    out=z[:],
+                    lhsT=h_codes[:, g, :].bitcast(FP8X4),
+                    lhsT_scale=h_scales[:, g, :],
+                    rhs=codes_of[unit][:, g, :].bitcast(FP8X4),
+                    rhs_scale=scales_of[unit][:, g, :],
+                    start=False,
+                    stop=(g == H_PASSES - 1),
+                )
+            z_of[unit] = z
+
+        def add_bias(unit):
+            z_biased = work.tile([P, N_TILE], F32)
+            nc.vector.tensor_tensor(
+                out=z_biased[:], in0=z_of[unit][:], in1=bias_of[unit][:], op=ALU.add
+            )
+            z_biased_of[unit] = z_biased
+
+        def activate(unit):
+            step, gate, first = unit_place(unit)
+            columns = slice(first, first + N_TILE)
+            if step == STEP_G:
+                nc.scalar.activation(out=cell[:, columns], in_=z_biased_of[unit][:], func=ACT.Tanh)
+            else:
+                gate_value = work.tile([P, N_TILE], F32)
+                nc.scalar.activation(out=gate_value[:], in_=z_biased_of[unit][:], func=ACT.Sigmoid)
+                gate_of[unit] = gate_value
+
+        def update_cell(unit):
+            step, gate, first = unit_place(unit)
+            columns = slice(first, first + N_TILE)
+            if step == STEP_I:
+                nc.vector.tensor_tensor(
+                    out=cell[:, columns], in0=gate_of[unit][:], in1=cell[:, columns], op=ALU.mult
+                )
+            if step == STEP_F:
+                kept = work.tile([P, N_TILE], F32)
+                nc.vector.tensor_tensor(
+                    out=kept[:], in0=gate_of[unit][:], in1=c_old[:, columns], op=ALU.mult
+                )
+                nc.vector.tensor_tensor(
+                    out=cell[:, columns], in0=kept[:], in1=cell[:, columns], op=ALU.add
+                )
+                nc.sync.dma_start(out=out_1[:, columns], in_=cell[:, columns])
+            if step == STEP_O:
+                h_new = work.tile([P, N_TILE], F32)
+                nc.vector.tensor_tensor(
+                    out=h_new[:], in0=gate_of[unit][:], in1=tanh_cell[:, columns], op=ALU.mult
+                )
+                nc.sync.dma_start(out=out_0[:, columns], in_=h_new[:])
+
+        def squash_cell(unit):
+            step, gate, first = unit_place(unit)
+            columns = slice(first, first + N_TILE)
+            if step == STEP_F:
+                nc.scalar.activation(out=tanh_cell[:, columns], in_=cell[:, columns], func=ACT.Tanh)
+
+        for piece in range(RAW_BUFS):
+            if piece == PIECES_PER_UNIT:
+                load_gate_weights(0)
+            load_piece(piece)
+        nc.sync.dma_start(out=c_old[:], in_=c_pre[:, :])
+
+        quantise_activations(h_raw, H_PASSES, h_codes, h_scales, h_grouped)
+        quantise_activations(x_raw, X_PASSES, x_codes, x_scales, x_grouped)
+
+        def prepare_gate_bias(step):
+            for unit in range(step * CHUNKS, (step + 1) * CHUNKS):
+                spread_bias(unit)
+            for unit in range(step * CHUNKS, (step + 1) * CHUNKS):
+                fetch_bias(unit)
+
+        def unit_due(r, lag):
+            unit, rest = divmod(r - lag, PIECES_PER_UNIT)
+            return unit if rest == 0 and 0 <= unit < UNITS else None
+
+        prepare_gate_bias(0)
+
+        for r in range(PIECES + 4):
+            unit = unit_due(r, 4)
+            if unit is not None:
+                activate(unit)
+            unit = unit_due(r, 5)
+            if unit is not None:
+                squash_cell(unit)
+            if 1 <= r <= PIECES:
+                quantise_piece(r - 1)
+            unit = unit_due(r, 3)
+            if unit is not None:
+                add_bias(unit)
+            unit = unit_due(r, 4)
+            if unit is not None:
+                update_cell(unit)
+            if r < PIECES:
+                transpose_piece(r)
+            unit = unit_due(r, 2)
+            if unit is not None:
+                multiply(unit)
+            if (r + 1) % PIECES_PER_GATE == 0 and r + 1 < PIECES:
+                prepare_gate_bias((r + 1) // PIECES_PER_GATE)
+            if r + RAW_BUFS < PIECES:
+                if (r + RAW_BUFS) % PIECES_PER_GATE == 0:
+                    load_gate_weights((r + RAW_BUFS) // PIECES_PER_GATE)
+                load_piece(r + RAW_BUFS)

@@ -25,6 +25,8 @@ WORDS_PER_PASS = K_PASS // 2
 N_TILE = 512
 CHUNKS = H // N_TILE
 UNITS = GATES * CHUNKS
+UNIT_BLOCKS = N_TILE // P
+BLOCKS = GATES * H // P
 ROWS_PER_PARTITION = 2
 PIECE_ROWS = P * ROWS_PER_PARTITION
 PIECES_PER_UNIT = N_TILE // PIECE_ROWS
@@ -34,9 +36,16 @@ PIECES_PER_GATE = PIECES // GATES
 GATE_ORDER = (3, 1, 0, 2)
 STEP_G, STEP_I, STEP_F, STEP_O = 0, 1, 2, 3
 
+C_ROUNDS = (3, 11, 19, 27)
+
+PREP_ROUND = 1
+ACTIVATIONS_BEFORE = 1
+WX_BEHIND = 1
+C_AFTER = 3
+SWAP_AHEAD = 1
+LAG_X, LAG_ACT, LAG_UPDATE, LAG_SQUASH, LAG_TURN, LAG_STORE = 3, 4, 5, 6, 6, 7
 RAW_BUFS = 8
 TRANSPOSE_BANKS = 7
-SCALAR_BANKS = 3
 
 FLOPS = 2 * P * (D + H) * GATES * H
 
@@ -48,37 +57,43 @@ def tile_lstmcell_w_e_kernel(
     with ExitStack() as ctx:
         ctx.enter_context(tc.manual_schedule())
         const = ctx.enter_context(tc.tile_pool(name="const", bufs=1))
+        swap_pool = ctx.enter_context(tc.tile_pool(name="swap", bufs=2))
         raw_pool = ctx.enter_context(tc.tile_pool(name="raw", bufs=RAW_BUFS))
-        grouped_pool = ctx.enter_context(tc.tile_pool(name="grouped", bufs=2 * H_PASSES))
+        grouped_pool = ctx.enter_context(tc.tile_pool(name="grouped", bufs=3 * H_PASSES))
         codes_pool = ctx.enter_context(tc.tile_pool(name="codes", bufs=2))
-        wx_pool = ctx.enter_context(tc.tile_pool(name="wx", bufs=2))
-        work = ctx.enter_context(tc.tile_pool(name="work", bufs=2))
-        bias_pool = ctx.enter_context(tc.tile_pool(name="bias", bufs=2 * CHUNKS))
+        wx_pool = ctx.enter_context(tc.tile_pool(name="wx", bufs=8))
+        work = ctx.enter_context(tc.tile_pool(name="work", bufs=3))
         banks = ctx.enter_context(tc.psum_pool(name="banks", bufs=TRANSPOSE_BANKS))
         z_pool = ctx.enter_context(tc.psum_pool(name="z", bufs=1))
 
         ident = const.tile([P, P], F32)
         make_identity(nc, ident[:])
 
-        bias_rows = const.tile([P, N_TILE], BF16)
-        nc.vector.memset(bias_rows[:], 0.0)
+        ident_bf16 = const.tile([P, P], BF16)
+        nc.vector.tensor_copy(out=ident_bf16[:], in_=ident[:])
+        bias_rows = const.tile([P, P], BF16)
         wx_planes = const.tile([P, GATES * X_PASSES, H], U8, align_bytes=64)
         nc.vector.memset(wx_planes[:].bitcast(I32), 0)
-        pick = const.tile([P, UNITS], BF16)
+        pick = const.tile([P, BLOCKS], BF16)
         nc.vector.tensor_tensor(
-            out=pick[:], in0=ident[:, 0:UNITS], in1=ident[:, UNITS : 2 * UNITS], op=ALU.add
+            out=pick[:], in0=ident[:, 0:BLOCKS], in1=ident[:, BLOCKS : 2 * BLOCKS], op=ALU.add
         )
 
         h_raw = const.tile([P, H], BF16)
-        nc.sync.dma_start(out=h_raw[:], in_=h_pre[:, :])
         x_raw = const.tile([P, D], BF16)
-        nc.sync.dma_start(out=x_raw[:], in_=x_t[:, :])
-        nc.sync.dma_start(
-            out=bias_rows[0:UNITS, :], in_=bW.rearrange("e (c n) -> (e c) n", n=N_TILE)
-        )
-        nc.sync.dma_start(
-            out=bias_rows[UNITS : 2 * UNITS, :], in_=bU.rearrange("e (c n) -> (e c) n", n=N_TILE)
-        )
+
+        def load_activations():
+            nc.sync.dma_start(out=h_raw[:], in_=h_pre[:, :])
+            nc.sync.dma_start(out=x_raw[:], in_=x_t[:, :])
+            nc.sync.dma_start(
+                out=bias_rows[0:BLOCKS, :], in_=bW.rearrange("e (c n) -> (e c) n", n=P)
+            )
+            nc.sync.dma_start(
+                out=bias_rows[BLOCKS : 2 * BLOCKS, :], in_=bU.rearrange("e (c n) -> (e c) n", n=P)
+            )
+
+        bias = const.tile([P, BLOCKS], F32)
+        c_raw = const.tile([P, H], BF16)
         c_old = const.tile([P, H], BF16)
 
         warm = const.tile([P, 1], F32)
@@ -92,52 +107,67 @@ def tile_lstmcell_w_e_kernel(
         codes_of = {}
         scales_of = {}
         wx_words_of = {}
-        bias_bank_of = {}
-        bias_of = {}
         z_of = {}
-        z_biased_of = {}
         gate_of = {}
+        h_new_of = {}
+        turned_of = {}
 
         def unit_place(unit):
-            step, chunk = divmod(unit, CHUNKS)
+            chunk, step = divmod(unit, GATES)
             return step, GATE_ORDER[step], chunk * N_TILE
 
         def load_piece(piece):
-            step, rest = divmod(piece, PIECES_PER_GATE)
-            rows = slice(rest * PIECE_ROWS, (rest + 1) * PIECE_ROWS)
-            raw = raw_pool.tile([P, ROWS_PER_PARTITION, H], BF16)
+            unit, half = divmod(piece, PIECES_PER_UNIT)
+            step, gate, first = unit_place(unit)
+            rows = slice(first + half * PIECE_ROWS, first + (half + 1) * PIECE_ROWS)
+            raw = raw_pool.tile([P, ROWS_PER_PARTITION * H], BF16)
             nc.sync.dma_start(
-                out=raw[:],
-                in_=Uh[GATE_ORDER[step], rows, :].rearrange(
-                    "(p t) k -> p t k", t=ROWS_PER_PARTITION
-                ),
+                out=raw[:].rearrange("p (t k) -> p t k", t=ROWS_PER_PARTITION),
+                in_=Uh[gate, rows, :].rearrange("(p t) k -> p t k", t=ROWS_PER_PARTITION),
             )
             raw_of[piece] = raw
 
-        def load_gate_weights(step):
-            first = GATE_ORDER[step] * X_PASSES
-            groups = slice(first, first + X_PASSES)
-            for quadrant in range(4):
-                nc.sync.dma_start(
-                    out=wx_planes[32 * quadrant : 32 * quadrant + 4, groups, :].bitcast(I32),
-                    in_=Wx_scales[groups, 4 * quadrant : 4 * quadrant + 4, :]
-                    .bitcast(I32)
-                    .rearrange("g r w -> r g w"),
-                )
-            wx_words = wx_pool.tile([P, X_PASSES, 2 * H], U8, align_bytes=64)
+        def load_weights(unit):
+            step, gate, first = unit_place(unit)
+            groups = slice(gate * X_PASSES, (gate + 1) * X_PASSES)
+            if unit < GATES:
+                for quadrant in range(4):
+                    nc.sync.dma_start(
+                        out=wx_planes[32 * quadrant : 32 * quadrant + 4, groups, :].bitcast(I32),
+                        in_=Wx_scales[groups, 4 * quadrant : 4 * quadrant + 4, :]
+                        .bitcast(I32)
+                        .rearrange("g r w -> r g w"),
+                    )
+            wx_words = wx_pool.tile([P, X_PASSES, 2 * N_TILE], U8, align_bytes=64)
             nc.sync.dma_start(
                 out=wx_words[:].bitcast(I32),
-                in_=Wx_words[groups, :, :].bitcast(I32).rearrange("g p w -> p g w"),
+                in_=Wx_words[groups, :, 2 * first : 2 * (first + N_TILE)]
+                .bitcast(I32)
+                .rearrange("g p w -> p g w"),
             )
-            wx_words_of[step] = wx_words
+            wx_words_of[unit] = wx_words
 
-        def quantise_activations(raw, passes, codes, scales, grouped):
+        def swap_steps(raw):
+            parts = raw[:].rearrange("p (c h m r j) -> p c h m r j", h=2, m=8, r=2, j=16)
+            spare = swap_pool.tile([P, raw[:].shape[1] // 4], BF16)
+            spare_parts = spare[:].rearrange("p (c m j) -> p c m j", m=8, j=16)
+            moves = (
+                (spare_parts, parts[:, :, 0, :, 1, :]),
+                (parts[:, :, 0, :, 1, :], parts[:, :, 1, :, 0, :]),
+                (parts[:, :, 1, :, 0, :], spare_parts),
+            )
+            return [
+                lambda to=to, source=source: nc.vector.tensor_copy(out=to, in_=source)
+                for to, source in moves
+            ]
+
+        def quantise_activations(raw, passes, word_columns, codes, scales, grouped):
             raw_words = raw[:].bitcast(F32)
             grouped_words = grouped[:].bitcast(F32).rearrange(
                 "q (g b u) -> q g b u", g=passes, u=2
             )
             for pair in range(passes // 2):
-                bank = banks.tile([P, 4, P], F32)
+                bank = banks.tile([P, 4, P], F32, name="bank")
                 for g in range(2):
                     for u in range(2):
                         nc.tensor.transpose(
@@ -162,29 +192,36 @@ def tile_lstmcell_w_e_kernel(
         x_scales = const.tile([P, X_PASSES, P], U8, align_bytes=64)
         x_grouped = const.tile([P, X_PASSES * P * 4], BF16, align_bytes=64)
 
-        def word_columns(g, u):
+        def h_word_columns(g, u):
+            first = WORDS_PER_PASS * g + P * u
+            return slice(first, first + P)
+
+        def x_word_columns(g, u):
             return slice(WORDS_PER_PASS * g + u, WORDS_PER_PASS * (g + 1), 2)
 
-        def transpose_piece(piece):
-            raw_words = raw_of[piece][:].bitcast(F32)
+        def transpose_piece(piece, after_first_copy):
+            raw_words = raw_of[piece][:].bitcast(F32).rearrange(
+                "p (t k) -> p t k", t=ROWS_PER_PARTITION
+            )
             for g in range(H_PASSES):
-                bank = banks.tile([P, 4, P], F32)
+                bank = banks.tile([P, 4, P], F32, name="bank")
                 for t in range(ROWS_PER_PARTITION):
                     for u in range(2):
                         nc.tensor.transpose(
                             out=bank[:, 2 * t + u, :],
-                            in_=raw_words[:, t, word_columns(g, u)],
+                            in_=raw_words[:, t, h_word_columns(g, u)],
                             identity=ident[:],
                         )
                 grouped = grouped_pool.tile([P, PIECE_ROWS * 4], BF16, align_bytes=64)
-                copy = nc.scalar.copy if g < SCALAR_BANKS else nc.vector.tensor_copy
-                copy(
+                nc.scalar.copy(
                     out=grouped[:].bitcast(F32).rearrange("q (p c) -> q p c", c=4),
                     in_=bank[:].rearrange("q c p -> q p c"),
                 )
                 grouped_of[(piece, g)] = grouped
+                if g == 0:
+                    after_first_copy()
 
-        def quantise_piece(piece):
+        def quantise_steps(piece):
             unit, half = divmod(piece, PIECES_PER_UNIT)
             if half == 0:
                 codes = codes_pool.tile([P, H_PASSES, N_TILE], U32, align_bytes=64)
@@ -192,72 +229,59 @@ def tile_lstmcell_w_e_kernel(
                 codes_of[unit] = codes
                 scales_of[unit] = scales
             columns = slice(half * PIECE_ROWS, (half + 1) * PIECE_ROWS)
-            for g in range(H_PASSES):
-                nc.vector.quantize_mx(
+            return [
+                lambda g=g: nc.vector.quantize_mx(
                     out=codes_of[unit][:, g, columns].bitcast(FP8X4),
                     scales=scales_of[unit][:, g, columns],
                     in_=grouped_of[(piece, g)][:],
                 )
-
-        def spread_bias(unit):
-            step, gate, first = unit_place(unit)
-            row = gate * CHUNKS + first // N_TILE
-            bank = banks.tile([P, 4, P], F32)
-            nc.tensor.matmul(
-                out=bank[:].rearrange("q c p -> q (c p)"),
-                lhsT=pick[:, row : row + 1].to_broadcast([P, P]),
-                rhs=bias_rows[:],
-                start=True,
-                stop=True,
-            )
-            bias_bank_of[unit] = bank
-
-        def fetch_bias(unit):
-            bias = bias_pool.tile([P, N_TILE], F32)
-            nc.scalar.copy(out=bias[:], in_=bias_bank_of[unit][:].rearrange("q c p -> q (c p)"))
-            bias_of[unit] = bias
+                for g in range(H_PASSES)
+            ]
 
         def multiply(unit):
             step, gate, first = unit_place(unit)
-            z = z_pool.tile([P, N_TILE], F32)
-            for g in range(X_PASSES):
-                nc.tensor.matmul_mx(
-                    out=z[:],
-                    lhsT=x_codes[:, g, :].bitcast(FP8X4),
-                    lhsT_scale=x_scales[:, g, :],
-                    rhs=wx_words_of[step][:, g, 2 * first : 2 * (first + N_TILE)].bitcast(FP4X4),
-                    rhs_scale=wx_planes[:, gate * X_PASSES + g, first : first + N_TILE],
-                    start=(g == 0),
-                    stop=False,
-                )
-            for g in range(H_PASSES):
-                nc.tensor.matmul_mx(
-                    out=z[:],
-                    lhsT=h_codes[:, g, :].bitcast(FP8X4),
-                    lhsT_scale=h_scales[:, g, :],
-                    rhs=codes_of[unit][:, g, :].bitcast(FP8X4),
-                    rhs_scale=scales_of[unit][:, g, :],
-                    start=False,
-                    stop=(g == H_PASSES - 1),
-                )
+            z = z_pool.tile([P, UNIT_BLOCKS, P], F32)
+            for b in range(UNIT_BLOCKS):
+                block = slice(first + b * P, first + (b + 1) * P)
+                for g in range(X_PASSES):
+                    nc.tensor.matmul_mx(
+                        out=z[:, b, :],
+                        lhsT=wx_words_of[unit][:, g, 2 * b * P : 2 * (b + 1) * P].bitcast(FP4X4),
+                        lhsT_scale=wx_planes[:, gate * X_PASSES + g, block],
+                        rhs=x_codes[:, g, :].bitcast(FP8X4),
+                        rhs_scale=x_scales[:, g, :],
+                        start=(g == 0),
+                        stop=False,
+                    )
+                for g in range(H_PASSES):
+                    columns = slice(b * P, (b + 1) * P)
+                    nc.tensor.matmul_mx(
+                        out=z[:, b, :],
+                        lhsT=codes_of[unit][:, g, columns].bitcast(FP8X4),
+                        lhsT_scale=scales_of[unit][:, g, columns],
+                        rhs=h_codes[:, g, :].bitcast(FP8X4),
+                        rhs_scale=h_scales[:, g, :],
+                        start=False,
+                        stop=(g == H_PASSES - 1),
+                    )
             z_of[unit] = z
-
-        def add_bias(unit):
-            z_biased = work.tile([P, N_TILE], F32)
-            nc.vector.tensor_tensor(
-                out=z_biased[:], in0=z_of[unit][:], in1=bias_of[unit][:], op=ALU.add
-            )
-            z_biased_of[unit] = z_biased
 
         def activate(unit):
             step, gate, first = unit_place(unit)
-            columns = slice(first, first + N_TILE)
             if step == STEP_G:
-                nc.scalar.activation(out=cell[:, columns], in_=z_biased_of[unit][:], func=ACT.Tanh)
+                value = cell[:, first : first + N_TILE]
             else:
                 gate_value = work.tile([P, N_TILE], F32)
-                nc.scalar.activation(out=gate_value[:], in_=z_biased_of[unit][:], func=ACT.Sigmoid)
                 gate_of[unit] = gate_value
+                value = gate_value[:]
+            for b in range(UNIT_BLOCKS):
+                row = (gate * H + first) // P + b
+                nc.scalar.activation(
+                    out=value[:, b * P : (b + 1) * P],
+                    in_=z_of[unit][:, b, :],
+                    func=ACT.Tanh if step == STEP_G else ACT.Sigmoid,
+                    bias=bias[:, row : row + 1],
+                )
 
         def update_cell(unit):
             step, gate, first = unit_place(unit)
@@ -274,13 +298,12 @@ def tile_lstmcell_w_e_kernel(
                 nc.vector.tensor_tensor(
                     out=cell[:, columns], in0=kept[:], in1=cell[:, columns], op=ALU.add
                 )
-                nc.sync.dma_start(out=out_1[:, columns], in_=cell[:, columns])
             if step == STEP_O:
                 h_new = work.tile([P, N_TILE], F32)
                 nc.vector.tensor_tensor(
                     out=h_new[:], in0=gate_of[unit][:], in1=tanh_cell[:, columns], op=ALU.mult
                 )
-                nc.sync.dma_start(out=out_0[:, columns], in_=h_new[:])
+                h_new_of[unit] = h_new
 
         def squash_cell(unit):
             step, gate, first = unit_place(unit)
@@ -288,50 +311,97 @@ def tile_lstmcell_w_e_kernel(
             if step == STEP_F:
                 nc.scalar.activation(out=tanh_cell[:, columns], in_=cell[:, columns], func=ACT.Tanh)
 
-        for piece in range(RAW_BUFS):
-            if piece == PIECES_PER_UNIT:
-                load_gate_weights(0)
+        def turn_result(unit):
+            step, gate, first = unit_place(unit)
+            if step in (STEP_F, STEP_O):
+                result = cell[:, first : first + N_TILE] if step == STEP_F else h_new_of[unit][:]
+                bank = banks.tile([P, 4, P], F32, name="bank")
+                for b in range(UNIT_BLOCKS):
+                    nc.tensor.transpose(
+                        out=bank[:, b, :], in_=result[:, b * P : (b + 1) * P], identity=ident[:]
+                    )
+                turned_of[unit] = bank
+
+        def store_result(unit):
+            step, gate, first = unit_place(unit)
+            if step in (STEP_F, STEP_O):
+                result = work.tile([P, N_TILE], F32)
+                nc.vector.tensor_copy(
+                    out=result[:], in_=turned_of[unit][:].rearrange("q c p -> q (c p)")
+                )
+                target = out_1 if step == STEP_F else out_0
+                nc.sync.dma_start(out=target[:, first : first + N_TILE], in_=result[:])
+
+        def turn_bias():
+            bank = banks.tile([P, BLOCKS], F32, name="bank")
+            nc.tensor.matmul(out=bank[:], lhsT=bias_rows[:], rhs=pick[:], start=True, stop=True)
+            nc.scalar.copy(out=bias[:], in_=bank[:])
+
+        def turn_c_pre(chunk):
+            bank = banks.tile([P, 4, P], BF16, name="bank")
+            for b in range(UNIT_BLOCKS):
+                first = chunk * N_TILE + b * P
+                nc.tensor.transpose(
+                    out=bank[:, b, :], in_=c_raw[:, first : first + P], identity=ident_bf16[:]
+                )
+            nc.scalar.copy(
+                out=c_old[:, chunk * N_TILE : (chunk + 1) * N_TILE],
+                in_=bank[:].rearrange("q c p -> q (c p)"),
+            )
+
+        def load_next(piece):
+            if piece == ACTIVATIONS_BEFORE:
+                load_activations()
             load_piece(piece)
-        nc.sync.dma_start(out=c_old[:], in_=c_pre[:, :])
+            if piece >= WX_BEHIND and (piece - WX_BEHIND) % PIECES_PER_UNIT == 0:
+                load_weights((piece - WX_BEHIND) // PIECES_PER_UNIT)
+            if piece == C_AFTER:
+                nc.sync.dma_start(out=c_raw[:], in_=c_pre[:, :])
 
-        quantise_activations(h_raw, H_PASSES, h_codes, h_scales, h_grouped)
-        quantise_activations(x_raw, X_PASSES, x_codes, x_scales, x_grouped)
+        for piece in range(RAW_BUFS):
+            load_next(piece)
 
-        def prepare_gate_bias(step):
-            for unit in range(step * CHUNKS, (step + 1) * CHUNKS):
-                spread_bias(unit)
-            for unit in range(step * CHUNKS, (step + 1) * CHUNKS):
-                fetch_bias(unit)
+        for piece in range(SWAP_AHEAD):
+            for step in swap_steps(raw_of[piece]):
+                step()
+
+        def prepare(r):
+            if r == PREP_ROUND:
+                quantise_activations(h_raw, H_PASSES, h_word_columns, h_codes, h_scales, h_grouped)
+            if r == PREP_ROUND + 1:
+                quantise_activations(x_raw, X_PASSES, x_word_columns, x_codes, x_scales, x_grouped)
+                turn_bias()
 
         def unit_due(r, lag):
             unit, rest = divmod(r - lag, PIECES_PER_UNIT)
             return unit if rest == 0 and 0 <= unit < UNITS else None
 
-        prepare_gate_bias(0)
+        def when_due(stage, r, lag):
+            unit = unit_due(r, lag)
+            if unit is not None:
+                stage(unit)
 
-        for r in range(PIECES + 4):
-            unit = unit_due(r, 4)
-            if unit is not None:
-                activate(unit)
-            unit = unit_due(r, 5)
-            if unit is not None:
-                squash_cell(unit)
-            if 1 <= r <= PIECES:
-                quantise_piece(r - 1)
-            unit = unit_due(r, 3)
-            if unit is not None:
-                add_bias(unit)
-            unit = unit_due(r, 4)
-            if unit is not None:
-                update_cell(unit)
+        for r in range(PIECES + LAG_STORE):
+            when_due(store_result, r, LAG_STORE)
+            when_due(update_cell, r, LAG_UPDATE)
+            quantises = quantise_steps(r - 1) if 1 <= r <= PIECES else []
+            swaps = swap_steps(raw_of[r + SWAP_AHEAD]) if r + SWAP_AHEAD < PIECES else []
+            for i in range(H_PASSES):
+                for steps in (swaps, quantises):
+                    if i < len(steps):
+                        steps[i]()
+            when_due(squash_cell, r, LAG_SQUASH)
+            if r == 0:
+                for step in swap_steps(h_raw):
+                    step()
             if r < PIECES:
-                transpose_piece(r)
-            unit = unit_due(r, 2)
-            if unit is not None:
-                multiply(unit)
-            if (r + 1) % PIECES_PER_GATE == 0 and r + 1 < PIECES:
-                prepare_gate_bias((r + 1) // PIECES_PER_GATE)
+                transpose_piece(r, lambda: when_due(activate, r, LAG_ACT))
+            else:
+                when_due(activate, r, LAG_ACT)
+            when_due(turn_result, r, LAG_TURN)
+            prepare(r)
+            if r in C_ROUNDS:
+                turn_c_pre(C_ROUNDS.index(r))
+            when_due(multiply, r, LAG_X)
             if r + RAW_BUFS < PIECES:
-                if (r + RAW_BUFS) % PIECES_PER_GATE == 0:
-                    load_gate_weights((r + RAW_BUFS) // PIECES_PER_GATE)
-                load_piece(r + RAW_BUFS)
+                load_next(r + RAW_BUFS)

@@ -30,6 +30,7 @@ BLOCKS = GATES * H // P
 ROWS_PER_PARTITION = 2
 PIECE_ROWS = P * ROWS_PER_PARTITION
 PIECES_PER_UNIT = N_TILE // PIECE_ROWS
+PIECE_BLOCKS = PIECE_ROWS // P
 PIECES = UNITS * PIECES_PER_UNIT
 PIECES_PER_GATE = PIECES // GATES
 
@@ -43,9 +44,9 @@ ACTIVATIONS_BEFORE = 1
 WX_BEHIND = 1
 C_AFTER = 3
 SWAP_AHEAD = 1
-LAG_X, LAG_ACT, LAG_UPDATE, LAG_SQUASH, LAG_TURN, LAG_STORE = 3, 4, 5, 6, 6, 7
+LAG_X, LAG_ACT, LAG_UPDATE, LAG_SQUASH, LAG_TURN, LAG_STORE = 2, 4, 5, 6, 6, 7
 RAW_BUFS = 8
-TRANSPOSE_BANKS = 7
+TRANSPOSE_BANKS = 6
 
 FLOPS = 2 * P * (D + H) * GATES * H
 
@@ -64,7 +65,7 @@ def tile_lstmcell_w_e_kernel(
         wx_pool = ctx.enter_context(tc.tile_pool(name="wx", bufs=8))
         work = ctx.enter_context(tc.tile_pool(name="work", bufs=3))
         banks = ctx.enter_context(tc.psum_pool(name="banks", bufs=TRANSPOSE_BANKS))
-        z_pool = ctx.enter_context(tc.psum_pool(name="z", bufs=1))
+        z_pool = ctx.enter_context(tc.psum_pool(name="z", bufs=2))
 
         ident = const.tile([P, P], F32)
         make_identity(nc, ident[:])
@@ -238,10 +239,14 @@ def tile_lstmcell_w_e_kernel(
                 for g in range(H_PASSES)
             ]
 
-        def multiply(unit):
+        def multiply(piece):
+            unit, half = divmod(piece, PIECES_PER_UNIT)
             step, gate, first = unit_place(unit)
-            z = z_pool.tile([P, UNIT_BLOCKS, P], F32)
-            for b in range(UNIT_BLOCKS):
+            if half == 0:
+                z = z_pool.tile([P, UNIT_BLOCKS, P], F32)
+                z_of[unit] = z
+            z = z_of[unit]
+            for b in range(half * PIECE_BLOCKS, (half + 1) * PIECE_BLOCKS):
                 block = slice(first + b * P, first + (b + 1) * P)
                 for g in range(X_PASSES):
                     nc.tensor.matmul_mx(
@@ -264,7 +269,6 @@ def tile_lstmcell_w_e_kernel(
                         start=False,
                         stop=(g == H_PASSES - 1),
                     )
-            z_of[unit] = z
 
         def activate(unit):
             step, gate, first = unit_place(unit)
@@ -402,6 +406,7 @@ def tile_lstmcell_w_e_kernel(
             prepare(r)
             if r in C_ROUNDS:
                 turn_c_pre(C_ROUNDS.index(r))
-            when_due(multiply, r, LAG_X)
+            if 0 <= r - LAG_X < PIECES:
+                multiply(r - LAG_X)
             if r + RAW_BUFS < PIECES:
                 load_next(r + RAW_BUFS)

@@ -22,31 +22,39 @@ X_PASSES = D // K_PASS
 H_PASSES = H // K_PASS
 WORDS_PER_PASS = K_PASS // 2
 
-N_TILE = 512
-CHUNKS = H // N_TILE
+CHUNK = 512
+CHUNK_BLOCKS = CHUNK // P
+CHUNKS = H // CHUNK
 UNITS = GATES * CHUNKS
-UNIT_BLOCKS = N_TILE // P
-BLOCKS = GATES * H // P
-ROWS_PER_PARTITION = 2
-PIECE_ROWS = P * ROWS_PER_PARTITION
-PIECES_PER_UNIT = N_TILE // PIECE_ROWS
-PIECE_BLOCKS = PIECE_ROWS // P
-PIECES = UNITS * PIECES_PER_UNIT
-PIECES_PER_GATE = PIECES // GATES
-
 GATE_ORDER = (3, 1, 0, 2)
 STEP_G, STEP_I, STEP_F, STEP_O = 0, 1, 2, 3
+BLOCKS = GATES * H // P
 
-C_ROUNDS = (3, 11, 19, 27)
+PIECES = [(unit, b, 2) for unit in range(UNITS) for b in (0, 2)][:-1] + [
+    (UNITS - 1, 2, 1),
+    (UNITS - 1, 3, 1),
+]
+GROUPS = [(unit, 0, CHUNK_BLOCKS) for unit in range(UNITS - 1)] + [
+    (UNITS - 1, 0, 2),
+    (UNITS - 1, 2, 1),
+    (UNITS - 1, 3, 1),
+]
 
 PREP_ROUND = 1
-ACTIVATIONS_BEFORE = 1
-WX_BEHIND = 1
-C_AFTER = 3
-SWAP_AHEAD = 1
-LAG_X, LAG_ACT, LAG_UPDATE, LAG_SQUASH, LAG_TURN, LAG_STORE = 2, 4, 5, 6, 6, 7
+C_AFTER = 5
+WX_LAST = 1
+SWAP_EARLY = {31: 29, 32: 30}
+V_BANKS = {30: (3,), 31: (1,), 32: (1,)}
+LAG_X = 2
+LAG_ACT, LAG_TURN, LAG_UPDATE, LAG_SQUASH = 3, 4, 5, 5
+TAIL_X = {}
+TAIL = {}
+ACTS_AFTER = 1
+WX_SHIFT = 1
+Q_FIRST = 6
 RAW_BUFS = 8
-TRANSPOSE_BANKS = 6
+TURN_BANKS = 6
+Z_BANKS = 2
 
 FLOPS = 2 * P * (D + H) * GATES * H
 
@@ -64,44 +72,33 @@ def tile_lstmcell_w_e_kernel(
         codes_pool = ctx.enter_context(tc.tile_pool(name="codes", bufs=2))
         wx_pool = ctx.enter_context(tc.tile_pool(name="wx", bufs=8))
         work = ctx.enter_context(tc.tile_pool(name="work", bufs=3))
-        banks = ctx.enter_context(tc.psum_pool(name="banks", bufs=TRANSPOSE_BANKS))
-        z_pool = ctx.enter_context(tc.psum_pool(name="z", bufs=2))
+        banks = ctx.enter_context(tc.psum_pool(name="banks", bufs=TURN_BANKS))
+        z_pool = ctx.enter_context(tc.psum_pool(name="z", bufs=Z_BANKS))
 
         ident = const.tile([P, P], F32)
         make_identity(nc, ident[:])
 
-        ident_bf16 = const.tile([P, P], BF16)
-        nc.vector.tensor_copy(out=ident_bf16[:], in_=ident[:])
-        bias_rows = const.tile([P, P], BF16)
         wx_planes = const.tile([P, GATES * X_PASSES, H], U8, align_bytes=64)
         nc.vector.memset(wx_planes[:].bitcast(I32), 0)
+        bias_rows = const.tile([P, P], BF16)
         pick = const.tile([P, BLOCKS], BF16)
         nc.vector.tensor_tensor(
             out=pick[:], in0=ident[:, 0:BLOCKS], in1=ident[:, BLOCKS : 2 * BLOCKS], op=ALU.add
         )
-
+        bias = const.tile([P, BLOCKS], F32)
         h_raw = const.tile([P, H], BF16)
         x_raw = const.tile([P, D], BF16)
-
-        def load_activations():
-            nc.sync.dma_start(out=h_raw[:], in_=h_pre[:, :])
-            nc.sync.dma_start(out=x_raw[:], in_=x_t[:, :])
-            nc.sync.dma_start(
-                out=bias_rows[0:BLOCKS, :], in_=bW.rearrange("e (c n) -> (e c) n", n=P)
-            )
-            nc.sync.dma_start(
-                out=bias_rows[BLOCKS : 2 * BLOCKS, :], in_=bU.rearrange("e (c n) -> (e c) n", n=P)
-            )
-
-        bias = const.tile([P, BLOCKS], F32)
-        c_raw = const.tile([P, H], BF16)
         c_old = const.tile([P, H], BF16)
 
         warm = const.tile([P, 1], F32)
         nc.scalar.activation(out=warm[:], in_=ident[:, 0:1], func=ACT.Sigmoid)
 
-        cell = const.tile([P, H], F32)
-        tanh_cell = const.tile([P, H], F32)
+        h_codes = const.tile([P, H_PASSES, P], U32, align_bytes=64)
+        h_scales = const.tile([P, H_PASSES, P], U8, align_bytes=64)
+        h_grouped = const.tile([P, H_PASSES * P * 4], BF16, align_bytes=64)
+        x_codes = const.tile([P, X_PASSES, P], U32, align_bytes=64)
+        x_scales = const.tile([P, X_PASSES, P], U8, align_bytes=64)
+        x_grouped = const.tile([P, X_PASSES * P * 4], BF16, align_bytes=64)
 
         raw_of = {}
         grouped_of = {}
@@ -110,21 +107,35 @@ def tile_lstmcell_w_e_kernel(
         wx_words_of = {}
         z_of = {}
         gate_of = {}
-        h_new_of = {}
+        product_of = {}
         turned_of = {}
+        tanh_of = {}
 
         def unit_place(unit):
             chunk, step = divmod(unit, GATES)
-            return step, GATE_ORDER[step], chunk * N_TILE
+            return step, GATE_ORDER[step], chunk * CHUNK
+
+        def group_columns(group):
+            unit, b0, blocks = group
+            step, gate, first = unit_place(unit)
+            return slice(first + b0 * P, first + (b0 + blocks) * P)
+
+        def load_activations():
+            nc.sync.dma_start(out=h_raw[:], in_=h_pre[:, :])
+            nc.sync.dma_start(out=x_raw[:], in_=x_t[:, :])
+            for rows, vector in ((slice(0, BLOCKS), bW), (slice(BLOCKS, 2 * BLOCKS), bU)):
+                nc.sync.dma_start(
+                    out=bias_rows[rows, :], in_=vector.rearrange("e (c n) -> (e c) n", n=P)
+                )
 
         def load_piece(piece):
-            unit, half = divmod(piece, PIECES_PER_UNIT)
+            unit, b, blocks = PIECES[piece]
             step, gate, first = unit_place(unit)
-            rows = slice(first + half * PIECE_ROWS, first + (half + 1) * PIECE_ROWS)
-            raw = raw_pool.tile([P, ROWS_PER_PARTITION * H], BF16)
+            rows = slice(first + b * P, first + (b + blocks) * P)
+            raw = raw_pool.tile([P, blocks * H], BF16)
             nc.sync.dma_start(
-                out=raw[:].rearrange("p (t k) -> p t k", t=ROWS_PER_PARTITION),
-                in_=Uh[gate, rows, :].rearrange("(p t) k -> p t k", t=ROWS_PER_PARTITION),
+                out=raw[:].rearrange("p (t k) -> p t k", t=blocks),
+                in_=Uh[gate, rows, :].rearrange("(p t) k -> p t k", t=blocks),
             )
             raw_of[piece] = raw
 
@@ -139,10 +150,10 @@ def tile_lstmcell_w_e_kernel(
                         .bitcast(I32)
                         .rearrange("g r w -> r g w"),
                     )
-            wx_words = wx_pool.tile([P, X_PASSES, 2 * N_TILE], U8, align_bytes=64)
+            wx_words = wx_pool.tile([P, X_PASSES, 2 * CHUNK], U8, align_bytes=64)
             nc.sync.dma_start(
                 out=wx_words[:].bitcast(I32),
-                in_=Wx_words[groups, :, 2 * first : 2 * (first + N_TILE)]
+                in_=Wx_words[groups, :, 2 * first : 2 * (first + CHUNK)]
                 .bitcast(I32)
                 .rearrange("g p w -> p g w"),
             )
@@ -162,13 +173,20 @@ def tile_lstmcell_w_e_kernel(
                 for to, source in moves
             ]
 
+        def h_word_columns(g, u):
+            first = WORDS_PER_PASS * g + P * u
+            return slice(first, first + P)
+
+        def x_word_columns(g, u):
+            return slice(WORDS_PER_PASS * g + u, WORDS_PER_PASS * (g + 1), 2)
+
         def quantise_activations(raw, passes, word_columns, codes, scales, grouped):
             raw_words = raw[:].bitcast(F32)
             grouped_words = grouped[:].bitcast(F32).rearrange(
                 "q (g b u) -> q g b u", g=passes, u=2
             )
             for pair in range(passes // 2):
-                bank = banks.tile([P, 4, P], F32, name="bank")
+                bank = banks.tile([P, 4, P], F32)
                 for g in range(2):
                     for u in range(2):
                         nc.tensor.transpose(
@@ -186,82 +204,80 @@ def tile_lstmcell_w_e_kernel(
                 in_=grouped[:],
             )
 
-        h_codes = const.tile([P, H_PASSES, P], U32, align_bytes=64)
-        h_scales = const.tile([P, H_PASSES, P], U8, align_bytes=64)
-        h_grouped = const.tile([P, H_PASSES * P * 4], BF16, align_bytes=64)
-        x_codes = const.tile([P, X_PASSES, P], U32, align_bytes=64)
-        x_scales = const.tile([P, X_PASSES, P], U8, align_bytes=64)
-        x_grouped = const.tile([P, X_PASSES * P * 4], BF16, align_bytes=64)
+        def turn_bias():
+            bank = banks.tile([P, BLOCKS], F32, name="bank")
+            nc.tensor.matmul(out=bank[:], lhsT=bias_rows[:], rhs=pick[:], start=True, stop=True)
+            nc.scalar.copy(out=bias[:], in_=bank[:])
 
-        def h_word_columns(g, u):
-            first = WORDS_PER_PASS * g + P * u
-            return slice(first, first + P)
+        def turn_steps(piece):
+            unit, b, blocks = PIECES[piece]
+            raw_words = raw_of[piece][:].bitcast(F32).rearrange("p (t k) -> p t k", t=blocks)
+            passes = 2 // blocks
 
-        def x_word_columns(g, u):
-            return slice(WORDS_PER_PASS * g + u, WORDS_PER_PASS * (g + 1), 2)
-
-        def transpose_piece(piece, after_first_copy):
-            raw_words = raw_of[piece][:].bitcast(F32).rearrange(
-                "p (t k) -> p t k", t=ROWS_PER_PARTITION
-            )
-            for g in range(H_PASSES):
-                bank = banks.tile([P, 4, P], F32, name="bank")
-                for t in range(ROWS_PER_PARTITION):
-                    for u in range(2):
-                        nc.tensor.transpose(
-                            out=bank[:, 2 * t + u, :],
-                            in_=raw_words[:, t, h_word_columns(g, u)],
-                            identity=ident[:],
-                        )
-                grouped = grouped_pool.tile([P, PIECE_ROWS * 4], BF16, align_bytes=64)
-                nc.scalar.copy(
-                    out=grouped[:].bitcast(F32).rearrange("q (p c) -> q p c", c=4),
-                    in_=bank[:].rearrange("q c p -> q p c"),
+            def step(i):
+                bank = banks.tile([P, 4, P], F32)
+                for j in range(passes):
+                    for t in range(blocks):
+                        for u in range(2):
+                            nc.tensor.transpose(
+                                out=bank[:, 2 * (j * blocks + t) + u, :],
+                                in_=raw_words[:, t, h_word_columns(i * passes + j, u)],
+                                identity=ident[:],
+                            )
+                grouped = grouped_pool.tile([P, passes, blocks * P * 4], BF16, align_bytes=64)
+                copy = nc.vector.tensor_copy if i in V_BANKS.get(piece, ()) else nc.scalar.copy
+                copy(
+                    out=grouped[:]
+                    .rearrange("q j n -> q (j n)")
+                    .bitcast(F32)
+                    .rearrange("q (j p c) -> q j p c", j=passes, c=2 * blocks),
+                    in_=bank[:].rearrange("q (j c) p -> q j p c", j=passes),
                 )
-                grouped_of[(piece, g)] = grouped
-                if g == 0:
-                    after_first_copy()
+                for j in range(passes):
+                    grouped_of[(piece, i * passes + j)] = grouped[:, j, :]
+
+            return [lambda i=i: step(i) for i in range(H_PASSES // passes)]
 
         def quantise_steps(piece):
-            unit, half = divmod(piece, PIECES_PER_UNIT)
-            if half == 0:
-                codes = codes_pool.tile([P, H_PASSES, N_TILE], U32, align_bytes=64)
-                scales = codes_pool.tile([P, H_PASSES, N_TILE], U8, align_bytes=64)
+            unit, b, blocks = PIECES[piece]
+            if b == 0:
+                codes = codes_pool.tile([P, H_PASSES, CHUNK], U32, align_bytes=64)
+                scales = codes_pool.tile([P, H_PASSES, CHUNK], U8, align_bytes=64)
                 codes_of[unit] = codes
                 scales_of[unit] = scales
-            columns = slice(half * PIECE_ROWS, (half + 1) * PIECE_ROWS)
+            columns = slice(b * P, (b + blocks) * P)
             return [
                 lambda g=g: nc.vector.quantize_mx(
                     out=codes_of[unit][:, g, columns].bitcast(FP8X4),
                     scales=scales_of[unit][:, g, columns],
-                    in_=grouped_of[(piece, g)][:],
+                    in_=grouped_of[(piece, g)],
                 )
                 for g in range(H_PASSES)
             ]
 
         def multiply(piece):
-            unit, half = divmod(piece, PIECES_PER_UNIT)
+            unit, b0, blocks = PIECES[piece]
             step, gate, first = unit_place(unit)
-            if half == 0:
-                z = z_pool.tile([P, UNIT_BLOCKS, P], F32)
+            if b0 == 0:
+                z = z_pool.tile([P, CHUNK_BLOCKS, P], F32)
                 z_of[unit] = z
-            z = z_of[unit]
-            for b in range(half * PIECE_BLOCKS, (half + 1) * PIECE_BLOCKS):
-                block = slice(first + b * P, first + (b + 1) * P)
+            for b in range(b0, b0 + blocks):
+                columns = slice(b * P, (b + 1) * P)
                 for g in range(X_PASSES):
                     nc.tensor.matmul_mx(
-                        out=z[:, b, :],
+                        out=z_of[unit][:, b, :],
                         lhsT=wx_words_of[unit][:, g, 2 * b * P : 2 * (b + 1) * P].bitcast(FP4X4),
-                        lhsT_scale=wx_planes[:, gate * X_PASSES + g, block],
+                        lhsT_scale=wx_planes[
+                            :, gate * X_PASSES + g, first + b * P : first + (b + 1) * P
+                        ],
                         rhs=x_codes[:, g, :].bitcast(FP8X4),
                         rhs_scale=x_scales[:, g, :],
                         start=(g == 0),
                         stop=False,
                     )
                 for g in range(H_PASSES):
-                    columns = slice(b * P, (b + 1) * P)
                     nc.tensor.matmul_mx(
-                        out=z[:, b, :],
+                        out=z_of[unit][:, b, :],
                         lhsT=codes_of[unit][:, g, columns].bitcast(FP8X4),
                         lhsT_scale=scales_of[unit][:, g, columns],
                         rhs=h_codes[:, g, :].bitcast(FP8X4),
@@ -270,143 +286,161 @@ def tile_lstmcell_w_e_kernel(
                         stop=(g == H_PASSES - 1),
                     )
 
-        def activate(unit):
+        def activate(group):
+            unit, b0, blocks = group
             step, gate, first = unit_place(unit)
-            if step == STEP_G:
-                value = cell[:, first : first + N_TILE]
-            else:
-                gate_value = work.tile([P, N_TILE], F32)
-                gate_of[unit] = gate_value
-                value = gate_value[:]
-            for b in range(UNIT_BLOCKS):
-                row = (gate * H + first) // P + b
+            gate_value = work.tile([P, blocks * P], F32, name=f"gate{step}")
+            for b in range(blocks):
+                row = (gate * H + first) // P + b0 + b
                 nc.scalar.activation(
-                    out=value[:, b * P : (b + 1) * P],
-                    in_=z_of[unit][:, b, :],
+                    out=gate_value[:, b * P : (b + 1) * P],
+                    in_=z_of[unit][:, b0 + b, :],
                     func=ACT.Tanh if step == STEP_G else ACT.Sigmoid,
                     bias=bias[:, row : row + 1],
                 )
+            gate_of[group] = gate_value
 
-        def update_cell(unit):
-            step, gate, first = unit_place(unit)
-            columns = slice(first, first + N_TILE)
-            if step == STEP_I:
-                nc.vector.tensor_tensor(
-                    out=cell[:, columns], in0=gate_of[unit][:], in1=cell[:, columns], op=ALU.mult
-                )
-            if step == STEP_F:
-                kept = work.tile([P, N_TILE], F32)
-                nc.vector.tensor_tensor(
-                    out=kept[:], in0=gate_of[unit][:], in1=c_old[:, columns], op=ALU.mult
-                )
-                nc.vector.tensor_tensor(
-                    out=cell[:, columns], in0=kept[:], in1=cell[:, columns], op=ALU.add
-                )
-            if step == STEP_O:
-                h_new = work.tile([P, N_TILE], F32)
-                nc.vector.tensor_tensor(
-                    out=h_new[:], in0=gate_of[unit][:], in1=tanh_cell[:, columns], op=ALU.mult
-                )
-                h_new_of[unit] = h_new
-
-        def squash_cell(unit):
-            step, gate, first = unit_place(unit)
-            columns = slice(first, first + N_TILE)
-            if step == STEP_F:
-                nc.scalar.activation(out=tanh_cell[:, columns], in_=cell[:, columns], func=ACT.Tanh)
-
-        def turn_result(unit):
-            step, gate, first = unit_place(unit)
-            if step in (STEP_F, STEP_O):
-                result = cell[:, first : first + N_TILE] if step == STEP_F else h_new_of[unit][:]
-                bank = banks.tile([P, 4, P], F32, name="bank")
-                for b in range(UNIT_BLOCKS):
-                    nc.tensor.transpose(
-                        out=bank[:, b, :], in_=result[:, b * P : (b + 1) * P], identity=ident[:]
-                    )
-                turned_of[unit] = bank
-
-        def store_result(unit):
-            step, gate, first = unit_place(unit)
-            if step in (STEP_F, STEP_O):
-                result = work.tile([P, N_TILE], F32)
-                nc.vector.tensor_copy(
-                    out=result[:], in_=turned_of[unit][:].rearrange("q c p -> q (c p)")
-                )
-                target = out_1 if step == STEP_F else out_0
-                nc.sync.dma_start(out=target[:, first : first + N_TILE], in_=result[:])
-
-        def turn_bias():
-            bank = banks.tile([P, BLOCKS], F32, name="bank")
-            nc.tensor.matmul(out=bank[:], lhsT=bias_rows[:], rhs=pick[:], start=True, stop=True)
-            nc.scalar.copy(out=bias[:], in_=bank[:])
-
-        def turn_c_pre(chunk):
-            bank = banks.tile([P, 4, P], BF16, name="bank")
-            for b in range(UNIT_BLOCKS):
-                first = chunk * N_TILE + b * P
+        def turn_back(value, blocks):
+            bank = banks.tile([P, 4, P], F32)
+            for b in range(blocks):
                 nc.tensor.transpose(
-                    out=bank[:, b, :], in_=c_raw[:, first : first + P], identity=ident_bf16[:]
+                    out=bank[:, b, :], in_=value[:, b * P : (b + 1) * P], identity=ident[:]
                 )
-            nc.scalar.copy(
-                out=c_old[:, chunk * N_TILE : (chunk + 1) * N_TILE],
-                in_=bank[:].rearrange("q c p -> q (c p)"),
-            )
+            return bank[:, 0:blocks, :].rearrange("q b p -> q (b p)")
+
+        def turn_group(group):
+            unit, b0, blocks = group
+            step, gate, first = unit_place(unit)
+            if step == STEP_F:
+                turned_of[(group, "f")] = turn_back(gate_of[group], blocks)
+                turned_of[(group, "ig")] = turn_back(product_of[unit - 1], blocks)
+            if step == STEP_O:
+                turned_of[(group, "o")] = turn_back(gate_of[group], blocks)
+
+        def input_product(group):
+            unit, b0, blocks = group
+            if unit_place(unit)[0] == STEP_I:
+                product = work.tile([P, CHUNK], F32)
+                nc.vector.tensor_tensor(
+                    out=product[:],
+                    in0=gate_of[group][:],
+                    in1=gate_of[(unit - 1, b0, blocks)][:],
+                    op=ALU.mult,
+                )
+                product_of[unit] = product
+
+        def update(group):
+            unit, b0, blocks = group
+            step, gate, first = unit_place(unit)
+            columns = group_columns(group)
+            if step == STEP_F:
+                kept = work.tile([P, CHUNK], F32)
+                nc.vector.tensor_tensor(
+                    out=kept[:], in0=turned_of[(group, "f")], in1=c_old[:, columns], op=ALU.mult
+                )
+                cell = work.tile([P, CHUNK], F32)
+                nc.vector.tensor_tensor(
+                    out=cell[:], in0=turned_of[(group, "ig")], in1=kept[:], op=ALU.add
+                )
+                nc.sync.dma_start(out=out_1[:, columns], in_=cell[:])
+                product_of[unit] = cell
+            if step == STEP_O:
+                h_new = work.tile([P, blocks * P], F32)
+                tanh_cell = tanh_of[unit - 1]
+                nc.vector.tensor_tensor(
+                    out=h_new[:],
+                    in0=turned_of[(group, "o")],
+                    in1=tanh_cell[:, b0 * P : (b0 + blocks) * P],
+                    op=ALU.mult,
+                )
+                nc.sync.dma_start(out=out_0[:, columns], in_=h_new[:])
+
+        def squash(group):
+            unit = group[0]
+            if unit_place(unit)[0] == STEP_F:
+                tanh_cell = work.tile([P, CHUNK], F32)
+                nc.scalar.activation(out=tanh_cell[:], in_=product_of[unit][:], func=ACT.Tanh)
+                tanh_of[unit] = tanh_cell
+
+        last_piece_of = {unit: i for i, (unit, b, blocks) in enumerate(PIECES)}
+
+        wx_after = {}
+        for unit in range(UNITS - WX_LAST):
+            wx_after.setdefault(last_piece_of[unit] + WX_SHIFT, []).append(unit)
 
         def load_next(piece):
-            if piece == ACTIVATIONS_BEFORE:
-                load_activations()
             load_piece(piece)
-            if piece >= WX_BEHIND and (piece - WX_BEHIND) % PIECES_PER_UNIT == 0:
-                load_weights((piece - WX_BEHIND) // PIECES_PER_UNIT)
+            if piece == ACTS_AFTER:
+                load_activations()
+            for unit in wx_after.get(piece, ()):
+                load_weights(unit)
             if piece == C_AFTER:
-                nc.sync.dma_start(out=c_raw[:], in_=c_pre[:, :])
+                nc.sync.dma_start(out=c_old[:], in_=c_pre[:, :])
+            if piece == len(PIECES) - 1:
+                for unit in range(UNITS - WX_LAST, UNITS):
+                    load_weights(unit)
 
         for piece in range(RAW_BUFS):
             load_next(piece)
 
-        for piece in range(SWAP_AHEAD):
-            for step in swap_steps(raw_of[piece]):
-                step()
+        schedule = {}
 
-        def prepare(r):
+        def plan(r, stage, what):
+            schedule.setdefault((r, stage), []).append(what)
+
+        def when_due(r, stage):
+            for what in schedule.get((r, stage), ()):
+                stage(what)
+
+        for piece in range(len(PIECES)):
+            plan(piece + TAIL_X.get(piece, LAG_X), multiply, piece)
+        for group in GROUPS:
+            unit, b0, blocks = group
+            ready = max(
+                i for i, (u, b, n) in enumerate(PIECES) if u == unit and b < b0 + blocks
+            )
+            lags = TAIL.get(group, (LAG_ACT, LAG_TURN, LAG_UPDATE, LAG_SQUASH))
+            plan(ready + lags[0], activate, group)
+            plan(ready + lags[1], input_product, group)
+            plan(ready + lags[1], turn_group, group)
+            plan(ready + lags[2], update, group)
+            plan(ready + lags[3], squash, group)
+        swap_round = {piece: SWAP_EARLY.get(piece, piece - 1) for piece in range(1, len(PIECES))}
+
+        for step in swap_steps(raw_of[0]):
+            step()
+        for r in range(max(key[0] for key in schedule) + 1):
+            when_due(r, update)
+            when_due(r, input_product)
+            quantises = quantise_steps(r - 1) if 1 <= r <= len(PIECES) else []
+            swaps = []
+            if r < Q_FIRST:
+                for step in quantises:
+                    step()
+                quantises = []
+            for piece in swap_round:
+                if swap_round[piece] == r:
+                    swaps += swap_steps(raw_of[piece])
+            for i in range(max(len(swaps), len(quantises))):
+                for steps in (swaps, quantises) if r >= Q_FIRST else (quantises, swaps):
+                    if i < len(steps):
+                        steps[i]()
+            if r == 0:
+                for step in swap_steps(h_raw):
+                    step()
+            for i, step in enumerate(turn_steps(r) if r < len(PIECES) else []):
+                step()
+                if i == 0:
+                    when_due(r, activate)
+            if r >= len(PIECES):
+                when_due(r, activate)
+            when_due(r, squash)
+            when_due(r, turn_group)
             if r == PREP_ROUND:
                 quantise_activations(h_raw, H_PASSES, h_word_columns, h_codes, h_scales, h_grouped)
             if r == PREP_ROUND + 1:
                 quantise_activations(x_raw, X_PASSES, x_word_columns, x_codes, x_scales, x_grouped)
                 turn_bias()
-
-        def unit_due(r, lag):
-            unit, rest = divmod(r - lag, PIECES_PER_UNIT)
-            return unit if rest == 0 and 0 <= unit < UNITS else None
-
-        def when_due(stage, r, lag):
-            unit = unit_due(r, lag)
-            if unit is not None:
-                stage(unit)
-
-        for r in range(PIECES + LAG_STORE):
-            when_due(store_result, r, LAG_STORE)
-            when_due(update_cell, r, LAG_UPDATE)
-            quantises = quantise_steps(r - 1) if 1 <= r <= PIECES else []
-            swaps = swap_steps(raw_of[r + SWAP_AHEAD]) if r + SWAP_AHEAD < PIECES else []
-            for i in range(H_PASSES):
-                for steps in (swaps, quantises):
-                    if i < len(steps):
-                        steps[i]()
-            when_due(squash_cell, r, LAG_SQUASH)
-            if r == 0:
-                for step in swap_steps(h_raw):
-                    step()
-            if r < PIECES:
-                transpose_piece(r, lambda: when_due(activate, r, LAG_ACT))
-            else:
-                when_due(activate, r, LAG_ACT)
-            when_due(turn_result, r, LAG_TURN)
-            prepare(r)
-            if r in C_ROUNDS:
-                turn_c_pre(C_ROUNDS.index(r))
-            if 0 <= r - LAG_X < PIECES:
-                multiply(r - LAG_X)
-            if r + RAW_BUFS < PIECES:
+            when_due(r, multiply)
+            if r + RAW_BUFS < len(PIECES):
                 load_next(r + RAW_BUFS)

@@ -30,7 +30,7 @@ GATE_ORDER = (3, 1, 0, 2)
 STEP_G, STEP_I, STEP_F, STEP_O = 0, 1, 2, 3
 BLOCKS = GATES * H // P
 
-PIECES = [(unit, b, 2) for unit in range(UNITS) for b in (0, 2)][:-1] + [
+PIECES = [(0, 0, 1), (0, 1, 1)] + [(unit, b, 2) for unit in range(UNITS) for b in (0, 2)][1:-1] + [
     (UNITS - 1, 2, 1),
     (UNITS - 1, 3, 1),
 ]
@@ -40,15 +40,28 @@ GROUPS = [(unit, 0, CHUNK_BLOCKS) for unit in range(UNITS - 1)] + [
     (UNITS - 1, 3, 1),
 ]
 
+PREP_V = False
 PREP_ROUND = 1
-C_AFTER = 5
+C_AFTER = 6
 WX_LAST = 1
-SWAP_EARLY = {31: 29, 32: 30}
-V_BANKS = {30: (3,), 31: (1,), 32: (1,)}
+SWAP_LEAD = 2
+LEAD_FROM = 9
+SWAP_EARLY = {}
+V_BANKS = dict(
+    [(piece, (3,)) for piece in range(12, 31, 4)] + [(31, (3,)), (32, (1,)), (33, (1,))]
+)
 LAG_X = 2
-LAG_ACT, LAG_TURN, LAG_UPDATE, LAG_SQUASH = 3, 4, 5, 5
-TAIL_X = {}
+LAG_ACT, LAG_TURN, LAG_UPDATE, LAG_SQUASH = 1, 2, 3, 3
+TAIL_X = 2
+TAIL_ROUND = 31
+RUN_BANKS = 4
+LAG_BLOCKS = 4
+ACT_BEHIND = 0
+SQ_BEHIND = 1
+TURN_BEHIND = 3
 TAIL = {}
+WARM_FIRST = 7
+WARM_ROUNDS = {0: 1, 1: 2, 2: 2, 3: 2}
 ACTS_AFTER = 1
 WX_SHIFT = 1
 Q_FIRST = 6
@@ -68,8 +81,8 @@ def tile_lstmcell_w_e_kernel(
         const = ctx.enter_context(tc.tile_pool(name="const", bufs=1))
         swap_pool = ctx.enter_context(tc.tile_pool(name="swap", bufs=2))
         raw_pool = ctx.enter_context(tc.tile_pool(name="raw", bufs=RAW_BUFS))
-        grouped_pool = ctx.enter_context(tc.tile_pool(name="grouped", bufs=3 * H_PASSES))
-        codes_pool = ctx.enter_context(tc.tile_pool(name="codes", bufs=2))
+        grouped_pool = ctx.enter_context(tc.tile_pool(name="grouped", bufs=3 * H_PASSES // 2))
+        codes_pool = ctx.enter_context(tc.tile_pool(name="codes", bufs=4))
         wx_pool = ctx.enter_context(tc.tile_pool(name="wx", bufs=8))
         work = ctx.enter_context(tc.tile_pool(name="work", bufs=3))
         banks = ctx.enter_context(tc.psum_pool(name="banks", bufs=TURN_BANKS))
@@ -89,6 +102,9 @@ def tile_lstmcell_w_e_kernel(
         h_raw = const.tile([P, H], BF16)
         x_raw = const.tile([P, D], BF16)
         c_old = const.tile([P, H], BF16)
+
+        zeros = const.tile([P, CHUNK], BF16)
+        nc.gpsimd.memset(zeros[:], 0.0)
 
         warm = const.tile([P, 1], F32)
         nc.scalar.activation(out=warm[:], in_=ident[:, 0:1], func=ACT.Sigmoid)
@@ -194,7 +210,7 @@ def tile_lstmcell_w_e_kernel(
                             in_=raw_words[:, word_columns(2 * pair + g, u)],
                             identity=ident[:],
                         )
-                nc.scalar.copy(
+                (nc.vector.tensor_copy if PREP_V else nc.scalar.copy)(
                     out=grouped_words[:, 2 * pair : 2 * pair + 2, :, :],
                     in_=bank[:].rearrange("q (g u) b -> q g b u", u=2),
                 )
@@ -209,60 +225,70 @@ def tile_lstmcell_w_e_kernel(
             nc.tensor.matmul(out=bank[:], lhsT=bias_rows[:], rhs=pick[:], start=True, stop=True)
             nc.scalar.copy(out=bias[:], in_=bank[:])
 
+        def keep_warm(times):
+            if times > 0:
+                bank = banks.tile([P, CHUNK], F32, name="bank")
+                for i in range(times):
+                    nc.tensor.matmul(
+                        out=bank[:], lhsT=zeros[:, 0:P], rhs=zeros[:], start=True, stop=True
+                    )
+
         def turn_steps(piece):
             unit, b, blocks = PIECES[piece]
             raw_words = raw_of[piece][:].bitcast(F32).rearrange("p (t k) -> p t k", t=blocks)
             passes = 2 // blocks
 
             def step(i):
+                first_pass = i * passes
+                if first_pass % 2 == 0:
+                    grouped = grouped_pool.tile([P, 2 * blocks * P * 4], BF16, align_bytes=64)
+                    grouped_of[(piece, first_pass // 2)] = grouped
                 bank = banks.tile([P, 4, P], F32)
                 for j in range(passes):
                     for t in range(blocks):
                         for u in range(2):
                             nc.tensor.transpose(
                                 out=bank[:, 2 * (j * blocks + t) + u, :],
-                                in_=raw_words[:, t, h_word_columns(i * passes + j, u)],
+                                in_=raw_words[:, t, h_word_columns(first_pass + j, u)],
                                 identity=ident[:],
                             )
-                grouped = grouped_pool.tile([P, passes, blocks * P * 4], BF16, align_bytes=64)
                 copy = nc.vector.tensor_copy if i in V_BANKS.get(piece, ()) else nc.scalar.copy
                 copy(
-                    out=grouped[:]
-                    .rearrange("q j n -> q (j n)")
+                    out=grouped_of[(piece, first_pass // 2)][:]
                     .bitcast(F32)
-                    .rearrange("q (j p c) -> q j p c", j=passes, c=2 * blocks),
+                    .rearrange("q (j p c) -> q j p c", j=2, c=2 * blocks)[
+                        :, first_pass % 2 : first_pass % 2 + passes, :, :
+                    ],
                     in_=bank[:].rearrange("q (j c) p -> q j p c", j=passes),
                 )
-                for j in range(passes):
-                    grouped_of[(piece, i * passes + j)] = grouped[:, j, :]
 
             return [lambda i=i: step(i) for i in range(H_PASSES // passes)]
 
         def quantise_steps(piece):
             unit, b, blocks = PIECES[piece]
-            if b == 0:
-                codes = codes_pool.tile([P, H_PASSES, CHUNK], U32, align_bytes=64)
-                scales = codes_pool.tile([P, H_PASSES, CHUNK], U8, align_bytes=64)
-                codes_of[unit] = codes
-                scales_of[unit] = scales
-            columns = slice(b * P, (b + blocks) * P)
-            return [
-                lambda g=g: nc.vector.quantize_mx(
-                    out=codes_of[unit][:, g, columns].bitcast(FP8X4),
-                    scales=scales_of[unit][:, g, columns],
-                    in_=grouped_of[(piece, g)],
-                )
-                for g in range(H_PASSES)
-            ]
+            codes = codes_pool.tile([P, H_PASSES, blocks * P], U32, align_bytes=64)
+            scales = codes_pool.tile([P, H_PASSES, blocks * P], U8, align_bytes=64)
+            codes_of[piece] = codes
+            scales_of[piece] = scales
 
-        def multiply(piece):
+            def step(pair):
+                passes = slice(2 * pair, 2 * pair + 2)
+                nc.vector.quantize_mx(
+                    out=codes[:, passes, :].rearrange("q g n -> q (g n)").bitcast(FP8X4),
+                    scales=scales[:, passes, :].rearrange("q g n -> q (g n)"),
+                    in_=grouped_of[(piece, pair)][:],
+                )
+
+            return [lambda pair=pair: step(pair) for pair in range(H_PASSES // 2)]
+
+        def multiply(piece, b):
             unit, b0, blocks = PIECES[piece]
             step, gate, first = unit_place(unit)
-            if b0 == 0:
+            if b == 0:
                 z = z_pool.tile([P, CHUNK_BLOCKS, P], F32)
                 z_of[unit] = z
-            for b in range(b0, b0 + blocks):
-                columns = slice(b * P, (b + 1) * P)
+            for b in (b,):
+                columns = slice((b - b0) * P, (b - b0 + 1) * P)
                 for g in range(X_PASSES):
                     nc.tensor.matmul_mx(
                         out=z_of[unit][:, b, :],
@@ -278,8 +304,8 @@ def tile_lstmcell_w_e_kernel(
                 for g in range(H_PASSES):
                     nc.tensor.matmul_mx(
                         out=z_of[unit][:, b, :],
-                        lhsT=codes_of[unit][:, g, columns].bitcast(FP8X4),
-                        lhsT_scale=scales_of[unit][:, g, columns],
+                        lhsT=codes_of[piece][:, g, columns].bitcast(FP8X4),
+                        lhsT_scale=scales_of[piece][:, g, columns],
                         rhs=h_codes[:, g, :].bitcast(FP8X4),
                         rhs_scale=h_scales[:, g, :],
                         start=False,
@@ -392,24 +418,36 @@ def tile_lstmcell_w_e_kernel(
             for what in schedule.get((r, stage), ()):
                 stage(what)
 
-        for piece in range(len(PIECES)):
-            plan(piece + TAIL_X.get(piece, LAG_X), multiply, piece)
-        for group in GROUPS:
-            unit, b0, blocks = group
-            ready = max(
-                i for i, (u, b, n) in enumerate(PIECES) if u == unit and b < b0 + blocks
-            )
-            lags = TAIL.get(group, (LAG_ACT, LAG_TURN, LAG_UPDATE, LAG_SQUASH))
-            plan(ready + lags[0], activate, group)
-            plan(ready + lags[1], input_product, group)
-            plan(ready + lags[1], turn_group, group)
-            plan(ready + lags[2], update, group)
-            plan(ready + lags[3], squash, group)
-        swap_round = {piece: SWAP_EARLY.get(piece, piece - 1) for piece in range(1, len(PIECES))}
+        product_blocks = [
+            (piece, b)
+            for piece, (unit, b0, blocks) in enumerate(PIECES)
+            for b in range(b0, b0 + blocks)
+        ]
+        progress = {"banks": 0, "products": 0}
 
+        def multiply_upto(limit, r):
+            while progress["products"] < min(limit, len(product_blocks)):
+                piece, b = product_blocks[progress["products"]]
+                multiply(piece, b)
+                progress["products"] = progress["products"] + 1
+                for group in GROUPS:
+                    unit, b0, blocks = group
+                    if unit == PIECES[piece][0] and b == b0 + blocks - 1:
+                        lags = TAIL.get(group, (LAG_ACT, LAG_TURN, LAG_UPDATE, LAG_SQUASH))
+                        plan(r + lags[0], activate, group)
+                        plan(r + lags[1], input_product, group)
+                        plan(r + lags[1], turn_group, group)
+                        plan(r + lags[2], update, group)
+                        plan(r + lags[3], squash, group)
+        swap_round = {
+            piece: max(0, SWAP_EARLY.get(piece, piece - (SWAP_LEAD if piece > LEAD_FROM else 1)))
+            for piece in range(1, len(PIECES))
+        }
+
+        keep_warm(WARM_FIRST)
         for step in swap_steps(raw_of[0]):
             step()
-        for r in range(max(key[0] for key in schedule) + 1):
+        for r in range(len(PIECES) + 6):
             when_due(r, update)
             when_due(r, input_product)
             quantises = quantise_steps(r - 1) if 1 <= r <= len(PIECES) else []
@@ -430,17 +468,26 @@ def tile_lstmcell_w_e_kernel(
                     step()
             for i, step in enumerate(turn_steps(r) if r < len(PIECES) else []):
                 step()
-                if i == 0:
+                if i == ACT_BEHIND:
                     when_due(r, activate)
+                if i == SQ_BEHIND:
+                    when_due(r, squash)
+                progress["banks"] = progress["banks"] + 1
+                if r < TAIL_ROUND and progress["banks"] % RUN_BANKS == 0:
+                    keep_warm(WARM_ROUNDS.get(r, 0))
+                    multiply_upto(progress["banks"] // 2 - LAG_BLOCKS, r)
+                if i == TURN_BEHIND:
+                    when_due(r, turn_group)
             if r >= len(PIECES):
                 when_due(r, activate)
-            when_due(r, squash)
-            when_due(r, turn_group)
+                when_due(r, squash)
+                when_due(r, turn_group)
             if r == PREP_ROUND:
                 quantise_activations(h_raw, H_PASSES, h_word_columns, h_codes, h_scales, h_grouped)
             if r == PREP_ROUND + 1:
                 quantise_activations(x_raw, X_PASSES, x_word_columns, x_codes, x_scales, x_grouped)
                 turn_bias()
-            when_due(r, multiply)
+            if r >= TAIL_ROUND:
+                multiply_upto(sum(PIECES[p][2] for p in range(min(len(PIECES), r - TAIL_X + 1))), r)
             if r + RAW_BUFS < len(PIECES):
                 load_next(r + RAW_BUFS)

@@ -40,32 +40,35 @@ GROUPS = [(unit, 0, CHUNK_BLOCKS) for unit in range(UNITS - 1)] + [
     (UNITS - 1, 3, 1),
 ]
 
-PREP_V = False
+SCALE_CHUNKS = 1
+H_SWAP_ROUND = 0
 PREP_ROUND = 1
-C_AFTER = 6
+C_AFTER = 8
 WX_LAST = 1
 SWAP_LEAD = 2
-LEAD_FROM = 9
+LEAD_FROM = 3
 SWAP_EARLY = {}
-V_BANKS = dict(
-    [(piece, (3,)) for piece in range(12, 31, 4)] + [(31, (3,)), (32, (1,)), (33, (1,))]
-)
-LAG_X = 2
-LAG_ACT, LAG_TURN, LAG_UPDATE, LAG_SQUASH = 1, 2, 3, 3
-TAIL_X = 2
+V_BANKS = {33: (1,)}
+TAIL_UNIT = 14
+I_PRODUCT = 3
+F_LAGS = (1, 2, 3, 3, 4, 4)
+O_LAGS = (1, 3, 4)
+F_TAIL = (1, 2, 3, 2, 3, 3)
+O_TAIL = (1, 2, 3)
+TAIL_X = 3
 TAIL_ROUND = 31
 RUN_BANKS = 4
 LAG_BLOCKS = 4
 ACT_BEHIND = 0
-SQ_BEHIND = 1
+SQ_BEHIND = 3
 TURN_BEHIND = 3
-TAIL = {}
-WARM_FIRST = 7
-WARM_ROUNDS = {0: 1, 1: 2, 2: 2, 3: 2}
 ACTS_AFTER = 1
-WX_SHIFT = 1
-Q_FIRST = 6
-RAW_BUFS = 8
+WX_SHIFT = 2
+Q_FIRST = 0
+WORK_BUFS = 3
+GROUPED_BUFS = 6
+CODES_BUFS = 4
+RAW_BUFS = 10
 TURN_BANKS = 6
 Z_BANKS = 2
 
@@ -79,12 +82,12 @@ def tile_lstmcell_w_e_kernel(
     with ExitStack() as ctx:
         ctx.enter_context(tc.manual_schedule())
         const = ctx.enter_context(tc.tile_pool(name="const", bufs=1))
-        swap_pool = ctx.enter_context(tc.tile_pool(name="swap", bufs=2))
+        swap_pool = ctx.enter_context(tc.tile_pool(name="swap", bufs=3))
         raw_pool = ctx.enter_context(tc.tile_pool(name="raw", bufs=RAW_BUFS))
-        grouped_pool = ctx.enter_context(tc.tile_pool(name="grouped", bufs=3 * H_PASSES // 2))
-        codes_pool = ctx.enter_context(tc.tile_pool(name="codes", bufs=4))
+        grouped_pool = ctx.enter_context(tc.tile_pool(name="grouped", bufs=GROUPED_BUFS))
+        codes_pool = ctx.enter_context(tc.tile_pool(name="codes", bufs=CODES_BUFS))
         wx_pool = ctx.enter_context(tc.tile_pool(name="wx", bufs=8))
-        work = ctx.enter_context(tc.tile_pool(name="work", bufs=3))
+        work = ctx.enter_context(tc.tile_pool(name="work", bufs=WORK_BUFS))
         banks = ctx.enter_context(tc.psum_pool(name="banks", bufs=TURN_BANKS))
         z_pool = ctx.enter_context(tc.psum_pool(name="z", bufs=Z_BANKS))
 
@@ -102,9 +105,6 @@ def tile_lstmcell_w_e_kernel(
         h_raw = const.tile([P, H], BF16)
         x_raw = const.tile([P, D], BF16)
         c_old = const.tile([P, H], BF16)
-
-        zeros = const.tile([P, CHUNK], BF16)
-        nc.gpsimd.memset(zeros[:], 0.0)
 
         warm = const.tile([P, 1], F32)
         nc.scalar.activation(out=warm[:], in_=ident[:, 0:1], func=ACT.Sigmoid)
@@ -126,6 +126,7 @@ def tile_lstmcell_w_e_kernel(
         product_of = {}
         turned_of = {}
         tanh_of = {}
+        kept_of = {}
 
         def unit_place(unit):
             chunk, step = divmod(unit, GATES)
@@ -158,11 +159,13 @@ def tile_lstmcell_w_e_kernel(
         def load_weights(unit):
             step, gate, first = unit_place(unit)
             groups = slice(gate * X_PASSES, (gate + 1) * X_PASSES)
-            if unit < GATES:
+            chunk = first // CHUNK
+            if chunk % SCALE_CHUNKS == 0:
+                columns = slice(first, first + SCALE_CHUNKS * CHUNK)
                 for quadrant in range(4):
                     nc.sync.dma_start(
-                        out=wx_planes[32 * quadrant : 32 * quadrant + 4, groups, :].bitcast(I32),
-                        in_=Wx_scales[groups, 4 * quadrant : 4 * quadrant + 4, :]
+                        out=wx_planes[32 * quadrant : 32 * quadrant + 4, groups, columns].bitcast(I32),
+                        in_=Wx_scales[groups, 4 * quadrant : 4 * quadrant + 4, columns]
                         .bitcast(I32)
                         .rearrange("g r w -> r g w"),
                     )
@@ -210,7 +213,7 @@ def tile_lstmcell_w_e_kernel(
                             in_=raw_words[:, word_columns(2 * pair + g, u)],
                             identity=ident[:],
                         )
-                (nc.vector.tensor_copy if PREP_V else nc.scalar.copy)(
+                nc.scalar.copy(
                     out=grouped_words[:, 2 * pair : 2 * pair + 2, :, :],
                     in_=bank[:].rearrange("q (g u) b -> q g b u", u=2),
                 )
@@ -224,14 +227,6 @@ def tile_lstmcell_w_e_kernel(
             bank = banks.tile([P, BLOCKS], F32, name="bank")
             nc.tensor.matmul(out=bank[:], lhsT=bias_rows[:], rhs=pick[:], start=True, stop=True)
             nc.scalar.copy(out=bias[:], in_=bank[:])
-
-        def keep_warm(times):
-            if times > 0:
-                bank = banks.tile([P, CHUNK], F32, name="bank")
-                for i in range(times):
-                    nc.tensor.matmul(
-                        out=bank[:], lhsT=zeros[:, 0:P], rhs=zeros[:], start=True, stop=True
-                    )
 
         def turn_steps(piece):
             unit, b, blocks = PIECES[piece]
@@ -334,59 +329,59 @@ def tile_lstmcell_w_e_kernel(
                 )
             return bank[:, 0:blocks, :].rearrange("q b p -> q (b p)")
 
-        def turn_group(group):
-            unit, b0, blocks = group
-            step, gate, first = unit_place(unit)
-            if step == STEP_F:
-                turned_of[(group, "f")] = turn_back(gate_of[group], blocks)
-                turned_of[(group, "ig")] = turn_back(product_of[unit - 1], blocks)
-            if step == STEP_O:
-                turned_of[(group, "o")] = turn_back(gate_of[group], blocks)
+        def turn_f(group):
+            turned_of[(group, "f")] = turn_back(gate_of[group], group[2])
+
+        def turn_ig(group):
+            turned_of[(group, "ig")] = turn_back(product_of[group[0] - 1], group[2])
+
+        def turn_o(group):
+            turned_of[(group, "o")] = turn_back(gate_of[group], group[2])
 
         def input_product(group):
             unit, b0, blocks = group
-            if unit_place(unit)[0] == STEP_I:
-                product = work.tile([P, CHUNK], F32)
-                nc.vector.tensor_tensor(
-                    out=product[:],
-                    in0=gate_of[group][:],
-                    in1=gate_of[(unit - 1, b0, blocks)][:],
-                    op=ALU.mult,
-                )
-                product_of[unit] = product
+            product = work.tile([P, CHUNK], F32)
+            nc.vector.tensor_tensor(
+                out=product[:],
+                in0=gate_of[group][:],
+                in1=gate_of[(unit - 1, b0, blocks)][:],
+                op=ALU.mult,
+            )
+            product_of[unit] = product
 
-        def update(group):
-            unit, b0, blocks = group
-            step, gate, first = unit_place(unit)
-            columns = group_columns(group)
-            if step == STEP_F:
-                kept = work.tile([P, CHUNK], F32)
-                nc.vector.tensor_tensor(
-                    out=kept[:], in0=turned_of[(group, "f")], in1=c_old[:, columns], op=ALU.mult
-                )
-                cell = work.tile([P, CHUNK], F32)
-                nc.vector.tensor_tensor(
-                    out=cell[:], in0=turned_of[(group, "ig")], in1=kept[:], op=ALU.add
-                )
-                nc.sync.dma_start(out=out_1[:, columns], in_=cell[:])
-                product_of[unit] = cell
-            if step == STEP_O:
-                h_new = work.tile([P, blocks * P], F32)
-                tanh_cell = tanh_of[unit - 1]
-                nc.vector.tensor_tensor(
-                    out=h_new[:],
-                    in0=turned_of[(group, "o")],
-                    in1=tanh_cell[:, b0 * P : (b0 + blocks) * P],
-                    op=ALU.mult,
-                )
-                nc.sync.dma_start(out=out_0[:, columns], in_=h_new[:])
+        def keep(group):
+            kept = work.tile([P, CHUNK], F32)
+            nc.vector.tensor_tensor(
+                out=kept[:],
+                in0=turned_of[(group, "f")],
+                in1=c_old[:, group_columns(group)],
+                op=ALU.mult,
+            )
+            kept_of[group] = kept
+
+        def add_cell(group):
+            cell = work.tile([P, CHUNK], F32)
+            nc.vector.tensor_tensor(
+                out=cell[:], in0=turned_of[(group, "ig")], in1=kept_of[group][:], op=ALU.add
+            )
+            nc.sync.dma_start(out=out_1[:, group_columns(group)], in_=cell[:])
+            product_of[group[0]] = cell
 
         def squash(group):
-            unit = group[0]
-            if unit_place(unit)[0] == STEP_F:
-                tanh_cell = work.tile([P, CHUNK], F32)
-                nc.scalar.activation(out=tanh_cell[:], in_=product_of[unit][:], func=ACT.Tanh)
-                tanh_of[unit] = tanh_cell
+            tanh_cell = work.tile([P, CHUNK], F32)
+            nc.scalar.activation(out=tanh_cell[:], in_=product_of[group[0]][:], func=ACT.Tanh)
+            tanh_of[group[0]] = tanh_cell
+
+        def finish(group):
+            unit, b0, blocks = group
+            h_new = work.tile([P, blocks * P], F32)
+            nc.vector.tensor_tensor(
+                out=h_new[:],
+                in0=turned_of[(group, "o")],
+                in1=tanh_of[unit - 1][:, b0 * P : (b0 + blocks) * P],
+                op=ALU.mult,
+            )
+            nc.sync.dma_start(out=out_0[:, group_columns(group)], in_=h_new[:])
 
         last_piece_of = {unit: i for i, (unit, b, blocks) in enumerate(PIECES)}
 
@@ -433,23 +428,33 @@ def tile_lstmcell_w_e_kernel(
                 for group in GROUPS:
                     unit, b0, blocks = group
                     if unit == PIECES[piece][0] and b == b0 + blocks - 1:
-                        lags = TAIL.get(group, (LAG_ACT, LAG_TURN, LAG_UPDATE, LAG_SQUASH))
-                        plan(r + lags[0], activate, group)
-                        plan(r + lags[1], input_product, group)
-                        plan(r + lags[1], turn_group, group)
-                        plan(r + lags[2], update, group)
-                        plan(r + lags[3], squash, group)
+                        step = unit_place(unit)[0]
+                        tail = unit >= TAIL_UNIT
+                        if step in (STEP_G, STEP_I):
+                            plan(r + 1, activate, group)
+                        if step == STEP_I:
+                            plan(r + I_PRODUCT, input_product, group)
+                        if step == STEP_F:
+                            for stage, lag in zip(
+                                (activate, turn_f, keep, turn_ig, add_cell, squash),
+                                F_TAIL if tail else F_LAGS,
+                            ):
+                                plan(r + lag, stage, group)
+                        if step == STEP_O:
+                            for stage, lag in zip(
+                                (activate, turn_o, finish), O_TAIL if tail else O_LAGS
+                            ):
+                                plan(r + lag, stage, group)
         swap_round = {
             piece: max(0, SWAP_EARLY.get(piece, piece - (SWAP_LEAD if piece > LEAD_FROM else 1)))
             for piece in range(1, len(PIECES))
         }
 
-        keep_warm(WARM_FIRST)
         for step in swap_steps(raw_of[0]):
             step()
-        for r in range(len(PIECES) + 6):
-            when_due(r, update)
-            when_due(r, input_product)
+        for r in range(len(PIECES) + 9):
+            for stage in (keep, add_cell, finish, input_product):
+                when_due(r, stage)
             quantises = quantise_steps(r - 1) if 1 <= r <= len(PIECES) else []
             swaps = []
             if r < Q_FIRST:
@@ -463,7 +468,7 @@ def tile_lstmcell_w_e_kernel(
                 for steps in (swaps, quantises) if r >= Q_FIRST else (quantises, swaps):
                     if i < len(steps):
                         steps[i]()
-            if r == 0:
+            if r == H_SWAP_ROUND:
                 for step in swap_steps(h_raw):
                     step()
             for i, step in enumerate(turn_steps(r) if r < len(PIECES) else []):
@@ -474,14 +479,15 @@ def tile_lstmcell_w_e_kernel(
                     when_due(r, squash)
                 progress["banks"] = progress["banks"] + 1
                 if r < TAIL_ROUND and progress["banks"] % RUN_BANKS == 0:
-                    keep_warm(WARM_ROUNDS.get(r, 0))
                     multiply_upto(progress["banks"] // 2 - LAG_BLOCKS, r)
                 if i == TURN_BEHIND:
-                    when_due(r, turn_group)
+                    for stage in (turn_o, turn_ig, turn_f):
+                        when_due(r, stage)
             if r >= len(PIECES):
                 when_due(r, activate)
                 when_due(r, squash)
-                when_due(r, turn_group)
+                for stage in (turn_o, turn_ig, turn_f):
+                    when_due(r, stage)
             if r == PREP_ROUND:
                 quantise_activations(h_raw, H_PASSES, h_word_columns, h_codes, h_scales, h_grouped)
             if r == PREP_ROUND + 1:

@@ -162,12 +162,12 @@ def tile_lstmcell_w_e_kernel(
             chunk = first // CHUNK
             if chunk % SCALE_CHUNKS == 0:
                 columns = slice(first, first + SCALE_CHUNKS * CHUNK)
-                for quadrant in range(4):
+                for r in range(4):
                     nc.sync.dma_start(
-                        out=wx_planes[32 * quadrant : 32 * quadrant + 4, groups, columns].bitcast(I32),
-                        in_=Wx_scales[groups, 4 * quadrant : 4 * quadrant + 4, columns]
+                        out=wx_planes[r : P : 32, groups, columns].bitcast(I32),
+                        in_=Wx_scales[groups, r : 16 : 4, columns]
                         .bitcast(I32)
-                        .rearrange("g r w -> r g w"),
+                        .rearrange("g q w -> q g w"),
                     )
             wx_words = wx_pool.tile([P, X_PASSES, 2 * CHUNK], U8, align_bytes=64)
             nc.sync.dma_start(
@@ -395,8 +395,10 @@ def tile_lstmcell_w_e_kernel(
                 load_activations()
             for unit in wx_after.get(piece, ()):
                 load_weights(unit)
-            if piece == C_AFTER:
-                nc.sync.dma_start(out=c_old[:], in_=c_pre[:, :])
+            for chunk in range(CHUNKS):
+                if piece == C_AFTER + chunk * GATES * 2:
+                    columns = slice(chunk * CHUNK, (chunk + 1) * CHUNK)
+                    nc.sync.dma_start(out=c_old[:, columns], in_=c_pre[:, columns])
             if piece == len(PIECES) - 1:
                 for unit in range(UNITS - WX_LAST, UNITS):
                     load_weights(unit)

from contextlib import ExitStack

import concourse.mybir as mybir
from concourse.masks import make_identity

F32 = mybir.dt.float32
BF16 = mybir.dt.bfloat16
I32 = mybir.dt.int32
U32 = mybir.dt.uint32
U8 = mybir.dt.uint8
FP8X4 = mybir.dt.float8_e4m3fn_x4
FP4X4 = mybir.dt.float4_e2m1fn_x4
ACT = mybir.ActivationFunctionType
ALU = mybir.AluOpType

P = 128
D = 1024
H = 2048
GATES = 4
K_PASS = 512
X_PASSES = D // K_PASS
H_PASSES = H // K_PASS
WORDS_PER_PASS = K_PASS // 2

CHUNK = 512
CHUNK_BLOCKS = CHUNK // P
CHUNKS = H // CHUNK
UNITS = GATES * CHUNKS
GATE_ORDER = (3, 1, 0, 2)
STEP_G, STEP_I, STEP_F, STEP_O = 0, 1, 2, 3
BLOCKS = GATES * H // P

PIECES = [(0, 0, 1), (0, 1, 1)] + [(unit, b, 2) for unit in range(UNITS) for b in (0, 2)][1:-1] + [
    (UNITS - 1, 2, 1),
    (UNITS - 1, 3, 1),
]
GROUPS = [(unit, 0, CHUNK_BLOCKS) for unit in range(UNITS - 1)] + [
    (UNITS - 1, 0, 2),
    (UNITS - 1, 2, 1),
    (UNITS - 1, 3, 1),
]

SCALE_CHUNKS = 1
H_SWAP_ROUND = 0
PREP_ROUND = 1
C_AFTER = 8
WX_LAST = 1
SWAP_LEAD = 2
LEAD_FROM = 3
SWAP_EARLY = {}
V_BANKS = {33: (1,)}
TAIL_UNIT = 14
I_PRODUCT = 3
F_LAGS = (1, 2, 3, 3, 4, 4)
O_LAGS = (1, 3, 4)
F_TAIL = (1, 2, 3, 2, 3, 3)
O_TAIL = (1, 2, 3)
TAIL_X = 3
TAIL_ROUND = 31
RUN_BANKS = 4
LAG_BLOCKS = 4
ACT_BEHIND = 0
SQ_BEHIND = 3
TURN_BEHIND = 3
ACTS_AFTER = 1
WX_SHIFT = 2
Q_FIRST = 0
WORK_BUFS = 3
GROUPED_BUFS = 6
CODES_BUFS = 4
RAW_BUFS = 10
TURN_BANKS = 6
Z_BANKS = 2

FLOPS = 2 * P * (D + H) * GATES * H


def tile_lstmcell_w_e_kernel(
    tc, x_t, h_pre, c_pre, Wx_words, Wx_scales, bW, Uh, bU, out_0, out_1
):
    nc = tc.nc
    with ExitStack() as ctx:
        ctx.enter_context(tc.manual_schedule())
        const = ctx.enter_context(tc.tile_pool(name="const", bufs=1))
        swap_pool = ctx.enter_context(tc.tile_pool(name="swap", bufs=3))
        raw_pool = ctx.enter_context(tc.tile_pool(name="raw", bufs=RAW_BUFS))
        grouped_pool = ctx.enter_context(tc.tile_pool(name="grouped", bufs=GROUPED_BUFS))
        codes_pool = ctx.enter_context(tc.tile_pool(name="codes", bufs=CODES_BUFS))
        wx_pool = ctx.enter_context(tc.tile_pool(name="wx", bufs=8))
        work = ctx.enter_context(tc.tile_pool(name="work", bufs=WORK_BUFS))
        banks = ctx.enter_context(tc.psum_pool(name="banks", bufs=TURN_BANKS))
        z_pool = ctx.enter_context(tc.psum_pool(name="z", bufs=Z_BANKS))

        ident = const.tile([P, P], F32)
        make_identity(nc, ident[:])

        wx_planes = const.tile([P, GATES * X_PASSES, H], U8, align_bytes=64)
        nc.vector.memset(wx_planes[:].bitcast(I32), 0)
        bias_rows = const.tile([P, P], BF16)
        pick = const.tile([P, BLOCKS], BF16)
        nc.vector.tensor_tensor(
            out=pick[:], in0=ident[:, 0:BLOCKS], in1=ident[:, BLOCKS : 2 * BLOCKS], op=ALU.add
        )
        bias = const.tile([P, BLOCKS], F32)
        h_raw = const.tile([P, H], BF16)
        x_raw = const.tile([P, D], BF16)
        c_old = const.tile([P, H], BF16)

        warm = const.tile([P, 1], F32)
        nc.scalar.activation(out=warm[:], in_=ident[:, 0:1], func=ACT.Sigmoid)

        h_codes = const.tile([P, H_PASSES, P], U32, align_bytes=64)
        h_scales = const.tile([P, H_PASSES, P], U8, align_bytes=64)
        h_grouped = const.tile([P, H_PASSES * P * 4], BF16, align_bytes=64)
        x_codes = const.tile([P, X_PASSES, P], U32, align_bytes=64)
        x_scales = const.tile([P, X_PASSES, P], U8, align_bytes=64)
        x_grouped = const.tile([P, X_PASSES * P * 4], BF16, align_bytes=64)

        raw_of = {}
        grouped_of = {}
        codes_of = {}
        scales_of = {}
        wx_words_of = {}
        z_of = {}
        gate_of = {}
        product_of = {}
        turned_of = {}
        tanh_of = {}
        kept_of = {}

        def unit_place(unit):
            chunk, step = divmod(unit, GATES)
            return step, GATE_ORDER[step], chunk * CHUNK

        def group_columns(group):
            unit, b0, blocks = group
            step, gate, first = unit_place(unit)
            return slice(first + b0 * P, first + (b0 + blocks) * P)

        def load_activations():
            nc.sync.dma_start(out=h_raw[:], in_=h_pre[:, :])
            nc.sync.dma_start(out=x_raw[:], in_=x_t[:, :])
            for rows, vector in ((slice(0, BLOCKS), bW), (slice(BLOCKS, 2 * BLOCKS), bU)):
                nc.sync.dma_start(
                    out=bias_rows[rows, :], in_=vector.rearrange("e (c n) -> (e c) n", n=P)
                )

        def load_piece(piece):
            unit, b, blocks = PIECES[piece]
            step, gate, first = unit_place(unit)
            rows = slice(first + b * P, first + (b + blocks) * P)
            raw = raw_pool.tile([P, blocks * H], BF16)
            nc.sync.dma_start(
                out=raw[:].rearrange("p (t k) -> p t k", t=blocks),
                in_=Uh[gate, rows, :].rearrange("(p t) k -> p t k", t=blocks),
            )
            raw_of[piece] = raw

        def load_weights(unit):
            step, gate, first = unit_place(unit)
            groups = slice(gate * X_PASSES, (gate + 1) * X_PASSES)
            chunk = first // CHUNK
            if chunk % SCALE_CHUNKS == 0:
                columns = slice(first, first + SCALE_CHUNKS * CHUNK)
                for r in range(4):
                    nc.sync.dma_start(
                        out=wx_planes[r : P : 32, groups, columns].bitcast(I32),
                        in_=Wx_scales[groups, r : 16 : 4, columns]
                        .bitcast(I32)
                        .rearrange("g q w -> q g w"),
                    )
            wx_words = wx_pool.tile([P, X_PASSES, 2 * CHUNK], U8, align_bytes=64)
            nc.sync.dma_start(
                out=wx_words[:].bitcast(I32),
                in_=Wx_words[groups, :, 2 * first : 2 * (first + CHUNK)]
                .bitcast(I32)
                .rearrange("g p w -> p g w"),
            )
            wx_words_of[unit] = wx_words

        def swap_steps(raw):
            parts = raw[:].rearrange("p (c h m r j) -> p c h m r j", h=2, m=8, r=2, j=16)
            spare = swap_pool.tile([P, raw[:].shape[1] // 4], BF16)
            spare_parts = spare[:].rearrange("p (c m j) -> p c m j", m=8, j=16)
            moves = (
                (spare_parts, parts[:, :, 0, :, 1, :]),
                (parts[:, :, 0, :, 1, :], parts[:, :, 1, :, 0, :]),
                (parts[:, :, 1, :, 0, :], spare_parts),
            )
            return [
                lambda to=to, source=source: nc.vector.tensor_copy(out=to, in_=source)
                for to, source in moves
            ]

        def h_word_columns(g, u):
            first = WORDS_PER_PASS * g + P * u
            return slice(first, first + P)

        def x_word_columns(g, u):
            return slice(WORDS_PER_PASS * g + u, WORDS_PER_PASS * (g + 1), 2)

        def quantise_activations(raw, passes, word_columns, codes, scales, grouped):
            raw_words = raw[:].bitcast(F32)
            grouped_words = grouped[:].bitcast(F32).rearrange(
                "q (g b u) -> q g b u", g=passes, u=2
            )
            for pair in range(passes // 2):
                bank = banks.tile([P, 4, P], F32)
                for g in range(2):
                    for u in range(2):
                        nc.tensor.transpose(
                            out=bank[:, 2 * g + u, :],
                            in_=raw_words[:, word_columns(2 * pair + g, u)],
                            identity=ident[:],
                        )
                nc.scalar.copy(
                    out=grouped_words[:, 2 * pair : 2 * pair + 2, :, :],
                    in_=bank[:].rearrange("q (g u) b -> q g b u", u=2),
                )
            nc.vector.quantize_mx(
                out=codes[:].rearrange("q g b -> q (g b)").bitcast(FP8X4),
                scales=scales[:].rearrange("q g b -> q (g b)"),
                in_=grouped[:],
            )

        def turn_bias():
            bank = banks.tile([P, BLOCKS], F32, name="bank")
            nc.tensor.matmul(out=bank[:], lhsT=bias_rows[:], rhs=pick[:], start=True, stop=True)
            nc.scalar.copy(out=bias[:], in_=bank[:])

        def turn_steps(piece):
            unit, b, blocks = PIECES[piece]
            raw_words = raw_of[piece][:].bitcast(F32).rearrange("p (t k) -> p t k", t=blocks)
            passes = 2 // blocks

            def step(i):
                first_pass = i * passes
                if first_pass % 2 == 0:
                    grouped = grouped_pool.tile([P, 2 * blocks * P * 4], BF16, align_bytes=64)
                    grouped_of[(piece, first_pass // 2)] = grouped
                bank = banks.tile([P, 4, P], F32)
                for j in range(passes):
                    for t in range(blocks):
                        for u in range(2):
                            nc.tensor.transpose(
                                out=bank[:, 2 * (j * blocks + t) + u, :],
                                in_=raw_words[:, t, h_word_columns(first_pass + j, u)],
                                identity=ident[:],
                            )
                copy = nc.vector.tensor_copy if i in V_BANKS.get(piece, ()) else nc.scalar.copy
                copy(
                    out=grouped_of[(piece, first_pass // 2)][:]
                    .bitcast(F32)
                    .rearrange("q (j p c) -> q j p c", j=2, c=2 * blocks)[
                        :, first_pass % 2 : first_pass % 2 + passes, :, :
                    ],
                    in_=bank[:].rearrange("q (j c) p -> q j p c", j=passes),
                )

            return [lambda i=i: step(i) for i in range(H_PASSES // passes)]

        def quantise_steps(piece):
            unit, b, blocks = PIECES[piece]
            codes = codes_pool.tile([P, H_PASSES, blocks * P], U32, align_bytes=64)
            scales = codes_pool.tile([P, H_PASSES, blocks * P], U8, align_bytes=64)
            codes_of[piece] = codes
            scales_of[piece] = scales

            def step(pair):
                passes = slice(2 * pair, 2 * pair + 2)
                nc.vector.quantize_mx(
                    out=codes[:, passes, :].rearrange("q g n -> q (g n)").bitcast(FP8X4),
                    scales=scales[:, passes, :].rearrange("q g n -> q (g n)"),
                    in_=grouped_of[(piece, pair)][:],
                )

            return [lambda pair=pair: step(pair) for pair in range(H_PASSES // 2)]

        def multiply(piece, b):
            unit, b0, blocks = PIECES[piece]
            step, gate, first = unit_place(unit)
            if b == 0:
                z = z_pool.tile([P, CHUNK_BLOCKS, P], F32)
                z_of[unit] = z
            for b in (b,):
                columns = slice((b - b0) * P, (b - b0 + 1) * P)
                for g in range(X_PASSES):
                    nc.tensor.matmul_mx(
                        out=z_of[unit][:, b, :],
                        lhsT=wx_words_of[unit][:, g, 2 * b * P : 2 * (b + 1) * P].bitcast(FP4X4),
                        lhsT_scale=wx_planes[
                            :, gate * X_PASSES + g, first + b * P : first + (b + 1) * P
                        ],
                        rhs=x_codes[:, g, :].bitcast(FP8X4),
                        rhs_scale=x_scales[:, g, :],
                        start=(g == 0),
                        stop=False,
                    )
                for g in range(H_PASSES):
                    nc.tensor.matmul_mx(
                        out=z_of[unit][:, b, :],
                        lhsT=codes_of[piece][:, g, columns].bitcast(FP8X4),
                        lhsT_scale=scales_of[piece][:, g, columns],
                        rhs=h_codes[:, g, :].bitcast(FP8X4),
                        rhs_scale=h_scales[:, g, :],
                        start=False,
                        stop=(g == H_PASSES - 1),
                    )

        def activate(group):
            unit, b0, blocks = group
            step, gate, first = unit_place(unit)
            gate_value = work.tile([P, blocks * P], F32, name=f"gate{step}")
            for b in range(blocks):
                row = (gate * H + first) // P + b0 + b
                nc.scalar.activation(
                    out=gate_value[:, b * P : (b + 1) * P],
                    in_=z_of[unit][:, b0 + b, :],
                    func=ACT.Tanh if step == STEP_G else ACT.Sigmoid,
                    bias=bias[:, row : row + 1],
                )
            gate_of[group] = gate_value

        def turn_back(value, blocks):
            bank = banks.tile([P, 4, P], F32)
            for b in range(blocks):
                nc.tensor.transpose(
                    out=bank[:, b, :], in_=value[:, b * P : (b + 1) * P], identity=ident[:]
                )
            return bank[:, 0:blocks, :].rearrange("q b p -> q (b p)")

        def turn_f(group):
            turned_of[(group, "f")] = turn_back(gate_of[group], group[2])

        def turn_ig(group):
            turned_of[(group, "ig")] = turn_back(product_of[group[0] - 1], group[2])

        def turn_o(group):
            turned_of[(group, "o")] = turn_back(gate_of[group], group[2])

        def input_product(group):
            unit, b0, blocks = group
            product = work.tile([P, CHUNK], F32)
            nc.vector.tensor_tensor(
                out=product[:],
                in0=gate_of[group][:],
                in1=gate_of[(unit - 1, b0, blocks)][:],
                op=ALU.mult,
            )
            product_of[unit] = product

        def keep(group):
            kept = work.tile([P, CHUNK], F32)
            nc.vector.tensor_tensor(
                out=kept[:],
                in0=turned_of[(group, "f")],
                in1=c_old[:, group_columns(group)],
                op=ALU.mult,
            )
            kept_of[group] = kept

        def add_cell(group):
            cell = work.tile([P, CHUNK], F32)
            nc.vector.tensor_tensor(
                out=cell[:], in0=turned_of[(group, "ig")], in1=kept_of[group][:], op=ALU.add
            )
            nc.sync.dma_start(out=out_1[:, group_columns(group)], in_=cell[:])
            product_of[group[0]] = cell

        def squash(group):
            tanh_cell = work.tile([P, CHUNK], F32)
            nc.scalar.activation(out=tanh_cell[:], in_=product_of[group[0]][:], func=ACT.Tanh)
            tanh_of[group[0]] = tanh_cell

        def finish(group):
            unit, b0, blocks = group
            h_new = work.tile([P, blocks * P], F32)
            nc.vector.tensor_tensor(
                out=h_new[:],
                in0=turned_of[(group, "o")],
                in1=tanh_of[unit - 1][:, b0 * P : (b0 + blocks) * P],
                op=ALU.mult,
            )
            nc.sync.dma_start(out=out_0[:, group_columns(group)], in_=h_new[:])

        last_piece_of = {unit: i for i, (unit, b, blocks) in enumerate(PIECES)}

        wx_after = {}
        for unit in range(UNITS - WX_LAST):
            wx_after.setdefault(last_piece_of[unit] + WX_SHIFT, []).append(unit)

        def load_next(piece):
            load_piece(piece)
            if piece == ACTS_AFTER:
                load_activations()
            for unit in wx_after.get(piece, ()):
                load_weights(unit)
            for chunk in range(CHUNKS):
                if piece == C_AFTER + chunk * GATES * 2:
                    columns = slice(chunk * CHUNK, (chunk + 1) * CHUNK)
                    nc.sync.dma_start(out=c_old[:, columns], in_=c_pre[:, columns])
            if piece == len(PIECES) - 1:
                for unit in range(UNITS - WX_LAST, UNITS):
                    load_weights(unit)

        for piece in range(RAW_BUFS):
            load_next(piece)

        schedule = {}

        def plan(r, stage, what):
            schedule.setdefault((r, stage), []).append(what)

        def when_due(r, stage):
            for what in schedule.get((r, stage), ()):
                stage(what)

        product_blocks = [
            (piece, b)
            for piece, (unit, b0, blocks) in enumerate(PIECES)
            for b in range(b0, b0 + blocks)
        ]
        progress = {"banks": 0, "products": 0}

        def multiply_upto(limit, r):
            while progress["products"] < min(limit, len(product_blocks)):
                piece, b = product_blocks[progress["products"]]
                multiply(piece, b)
                progress["products"] = progress["products"] + 1
                for group in GROUPS:
                    unit, b0, blocks = group
                    if unit == PIECES[piece][0] and b == b0 + blocks - 1:
                        step = unit_place(unit)[0]
                        tail = unit >= TAIL_UNIT
                        if step in (STEP_G, STEP_I):
                            plan(r + 1, activate, group)
                        if step == STEP_I:
                            plan(r + I_PRODUCT, input_product, group)
                        if step == STEP_F:
                            for stage, lag in zip(
                                (activate, turn_f, keep, turn_ig, add_cell, squash),
                                F_TAIL if tail else F_LAGS,
                            ):
                                plan(r + lag, stage, group)
                        if step == STEP_O:
                            for stage, lag in zip(
                                (activate, turn_o, finish), O_TAIL if tail else O_LAGS
                            ):
                                plan(r + lag, stage, group)
        swap_round = {
            piece: max(0, SWAP_EARLY.get(piece, piece - (SWAP_LEAD if piece > LEAD_FROM else 1)))
            for piece in range(1, len(PIECES))
        }

        for step in swap_steps(raw_of[0]):
            step()
        for r in range(len(PIECES) + 9):
            for stage in (keep, add_cell, finish, input_product):
                when_due(r, stage)
            quantises = quantise_steps(r - 1) if 1 <= r <= len(PIECES) else []
            swaps = []
            if r < Q_FIRST:
                for step in quantises:
                    step()
                quantises = []
            for piece in swap_round:
                if swap_round[piece] == r:
                    swaps += swap_steps(raw_of[piece])
            for i in range(max(len(swaps), len(quantises))):
                for steps in (swaps, quantises) if r >= Q_FIRST else (quantises, swaps):
                    if i < len(steps):
                        steps[i]()
            if r == H_SWAP_ROUND:
                for step in swap_steps(h_raw):
                    step()
            for i, step in enumerate(turn_steps(r) if r < len(PIECES) else []):
                step()
                if i == ACT_BEHIND:
                    when_due(r, activate)
                if i == SQ_BEHIND:
                    when_due(r, squash)
                progress["banks"] = progress["banks"] + 1
                if r < TAIL_ROUND and progress["banks"] % RUN_BANKS == 0:
                    multiply_upto(progress["banks"] // 2 - LAG_BLOCKS, r)
                if i == TURN_BEHIND:
                    for stage in (turn_o, turn_ig, turn_f):
                        when_due(r, stage)
            if r >= len(PIECES):
                when_due(r, activate)
                when_due(r, squash)
                for stage in (turn_o, turn_ig, turn_f):
                    when_due(r, stage)
            if r == PREP_ROUND:
                quantise_activations(h_raw, H_PASSES, h_word_columns, h_codes, h_scales, h_grouped)
            if r == PREP_ROUND + 1:
                quantise_activations(x_raw, X_PASSES, x_word_columns, x_codes, x_scales, x_grouped)
                turn_bias()
            if r >= TAIL_ROUND:
                multiply_upto(sum(PIECES[p][2] for p in range(min(len(PIECES), r - TAIL_X + 1))), r)
            if r + RAW_BUFS < len(PIECES):
                load_next(r + RAW_BUFS)
